import numpy as np
import ml_dtypes


def mxq(x, axis, fmt="e4m3"):
    dtype, down = {"e4m3": (ml_dtypes.float8_e4m3fn, 7), "e5m2": (ml_dtypes.float8_e5m2, 14)}[fmt]
    v = np.moveaxis(np.asarray(x, np.float32).astype(ml_dtypes.bfloat16).astype(np.float64), axis, -1)
    blocks = v.reshape(v.shape[:-1] + (-1, 32))
    amax = np.abs(blocks).max(-1, keepdims=True)
    byte = np.maximum(np.where(amax > 0, np.frexp(amax)[1] - 1 + 127, 0) - down, 1)
    scale = np.exp2(byte - 127.0)
    codes = (blocks / scale).astype(np.float32).astype(dtype).astype(np.float64)
    return np.moveaxis((codes * scale).reshape(v.shape), -1, axis)


WIDE = False


def mx_kscale(k):
    if not WIDE:
        return np.ones(k)
    levels = np.array([10, -10, 5, -5, 0])
    a = np.random.permutation(np.resize(levels, k // 512 * 4)).reshape(k // 512, 4)
    idx = np.arange(k)
    return np.exp2(a[idx // 512, idx % 128 // 32])


BF16 = ml_dtypes.bfloat16


def bf(x):
    return np.asarray(x, np.float32).astype(BF16)


def f64(x):
    return np.asarray(x).astype(np.float64)


N, MI0, MI1, MS, MG, MO0, MO1, DV = 256, 1024, 512, 2048, 1024, 1024, 512, 3
EPS = 1e-5


def irlin_mx(x, mul0, mul1, w0, w1):
    n = x.shape[0]
    x0 = x[:, :mul0]
    x1 = x[:, mul0:].reshape(n, mul1, DV).transpose(0, 2, 1)
    y0 = (mxq(x0, 1, "e4m3") @ mxq(w0, 0, "e4m3")) * (1.0 / np.sqrt(mul0))
    y1 = (mxq(x1, 2, "e4m3") @ mxq(w1, 0, "e4m3")).transpose(0, 2, 1) * (1.0 / np.sqrt(mul1))
    return np.concatenate([y0, y1.reshape(n, -1)], axis=-1)


def irlin_plain(x, mul0, mul1, w0, w1):
    n = x.shape[0]
    x0 = x[:, :mul0]
    x1 = x[:, mul0:].reshape(n, mul1, DV).transpose(0, 2, 1)
    y0 = (x0 @ w0) * (1.0 / np.sqrt(mul0))
    y1 = (x1 @ w1).transpose(0, 2, 1) * (1.0 / np.sqrt(mul1))
    return np.concatenate([y0, y1.reshape(n, -1)], axis=-1)


def batchnorm(x, w, b):
    n = x.shape[0]
    s = x[:, :MO0]
    v = x[:, MO0:].reshape(n, MO1, DV)
    s = s - s.mean(0)
    s_inv = 1.0 / np.sqrt((s * s).mean(0) + EPS)
    s = s * (s_inv * w[:MO0]) + b
    v_inv = 1.0 / np.sqrt((v * v).mean(-1).mean(0) + EPS)
    v = v * (v_inv * w[MO0:])[None, :, None]
    return np.concatenate([s, v.reshape(n, -1)], axis=-1)


def setup_inputs():
    s0, s1 = mx_kscale(MS), mx_kscale(MG)
    h0 = (0.1 + 0.3 * np.random.standard_normal((N, MS))) * s0
    h1 = 0.28 * np.random.standard_normal((N, MG, DV)) * s1[None, :, None]
    return {"h2": bf(np.concatenate([h0, h1.reshape(N, -1)], axis=-1)),
            "features": bf(np.random.standard_normal((N, MI0 + DV * MI1))),
            "lin3_W0": bf(np.random.standard_normal((MS, MO0)) / s0[:, None]),
            "lin3_W1": bf(np.random.standard_normal((MG, MO1)) / s1[:, None]),
            "byp_W0": bf(np.random.standard_normal((MI0, MO0))),
            "byp_W1": bf(np.random.standard_normal((MI1, MO1))),
            "bn_weight": bf(1.0 + 0.1 * np.random.standard_normal(MO0 + MO1)),
            "bn_bias": bf(0.1 * np.random.standard_normal(MO0))}


def reference(h2, features, lin3_W0, lin3_W1, byp_W0, byp_W1, bn_weight, bn_bias):
    out = irlin_mx(f64(h2), MS, MG, f64(lin3_W0), f64(lin3_W1))
    out = out + irlin_plain(f64(features), MI0, MI1, f64(byp_W0), f64(byp_W1))
    return batchnorm(out, f64(bn_weight), f64(bn_bias))

@@ -1,0 +1,357 @@
+from contextlib import ExitStack
+
+import concourse.mybir as mybir
+from concourse.masks import make_identity
+
+F32 = mybir.dt.float32
+BF16 = mybir.dt.bfloat16
+U32 = mybir.dt.uint32
+U8 = mybir.dt.uint8
+FP8X4 = mybir.dt.float8_e4m3fn_x4
+ACT = mybir.ActivationFunctionType
+ALU = mybir.AluOpType
+
+P = 128
+NODES = 256
+NODE_TILES = NODES // P
+DV = 3
+H_SCAL, H_VEC = 2048, 1024
+F_SCAL, F_VEC = 1024, 512
+O_SCAL, O_VEC = 1024, 512
+EPS = 1e-5
+
+PACK = 4
+K_PASS = P * PACK
+PAIR = 2
+K_WORDS = P * PAIR
+
+S_PASSES = H_SCAL // K_PASS
+V_PASSES = H_VEC // K_PASS
+S_TILES = O_SCAL // P
+V_TILES = O_VEC // P
+FS_UNITS = F_SCAL // K_WORDS
+FV_BLOCKS = F_VEC // K_WORDS
+
+SCALAR_SHARE = 4
+
+FLOPS = 2 * NODES * (H_SCAL + F_SCAL) * O_SCAL + 2 * NODES * DV * (H_VEC + F_VEC) * O_VEC
+
+
+def quantise_weight_pass(nc, stage, raw, codes, scales):
+    width = raw.shape[2]
+    grouped = stage.tile([P, width, PACK], BF16, align_bytes=64, tag="w_grouped")
+    split = width - width // SCALAR_SHARE
+    nc.vector.tensor_copy(
+        out=grouped[:, :split, :].rearrange("p (c i) t -> p c t i", i=4),
+        in_=raw[:, :, :split].rearrange("p t (c i) -> p c t i", i=4),
+    )
+    nc.scalar.copy(
+        out=grouped[:, split:, :].rearrange("p (c i) t -> p c t i", i=4),
+        in_=raw[:, :, split:].rearrange("p t (c i) -> p c t i", i=4),
+    )
+    nc.vector.quantize_mx(
+        out=codes.bitcast(FP8X4),
+        scales=scales,
+        in_=grouped[:].rearrange("p c t -> p (c t)"),
+    )
+
+
+def transpose_words(nc, bank, slot, words_of_tile, ident):
+    for nt in range(NODE_TILES):
+        nc.tensor.transpose(bank[:, slot, nt * P : (nt + 1) * P], words_of_tile(nt), ident[:])
+
+
+def tile_feedforward_pb_kernel(
+    tc, h2, features, lin3_W0, lin3_W1, byp_W0, byp_W1, bn_weight, bn_bias, out
+):
+    nc = tc.nc
+    with ExitStack() as ctx:
+        const = ctx.enter_context(tc.tile_pool(name="const", bufs=1))
+        keep = ctx.enter_context(tc.tile_pool(name="keep", bufs=1))
+        stage = ctx.enter_context(tc.tile_pool(name="stage", bufs=2))
+        small = ctx.enter_context(tc.tile_pool(name="small", bufs=1))
+        psum_in = ctx.enter_context(tc.psum_pool(name="psum_in", bufs=2))
+        psum_acc = ctx.enter_context(tc.psum_pool(name="psum_acc", bufs=4))
+        psum_back = ctx.enter_context(tc.psum_pool(name="psum_back", bufs=2))
+
+        ident = const.tile([P, P], F32)
+        make_identity(nc, ident[:])
+        eps = const.tile([P, 1], F32)
+        nc.vector.memset(eps[:], EPS)
+        warm = const.tile([P, 1], F32)
+        nc.scalar.activation(out=warm[:], in_=eps[:], func=ACT.Sqrt)
+
+        fv_raw = keep.tile([P, NODE_TILES, DV * F_VEC], BF16)
+        fs_raw = keep.tile([P, NODE_TILES, F_SCAL], BF16)
+        hv_raw = keep.tile([P, NODE_TILES, DV * H_VEC], BF16)
+        hs_raw = keep.tile([P, NODE_TILES, H_SCAL], BF16)
+        b1 = keep.tile([P, FV_BLOCKS, PAIR, O_VEC], BF16)
+        b0 = keep.tile([P, FS_UNITS, PAIR, O_SCAL], BF16)
+        w1_raw = keep.tile([P, V_PASSES, PACK, O_VEC], BF16)
+        w0_raw = keep.tile([P, S_PASSES, PACK, O_SCAL], BF16)
+
+        W_ROWS = (O_SCAL + O_VEC) // P
+        B_ROWS = O_SCAL // P
+        bn_rows = const.tile([P, P], BF16)
+        nc.vector.memset(bn_rows[:], 0.0)
+        nc.sync.dma_start(out=bn_rows[0:W_ROWS, :], in_=bn_weight.rearrange("(r c) -> r c", c=P))
+        nc.sync.dma_start(out=bn_rows[W_ROWS : W_ROWS + B_ROWS, :], in_=bn_bias.rearrange("(r c) -> r c", c=P))
+
+        for nt in range(NODE_TILES):
+            nc.sync.dma_start(out=fv_raw[:, nt, :], in_=features[nt * P : (nt + 1) * P, F_SCAL:])
+        nc.sync.dma_start(
+            out=b1[:].rearrange("p b e o -> p b (e o)"),
+            in_=byp_W1.rearrange("(b p e) o -> p b (e o)", p=P, e=PAIR),
+        )
+        nc.sync.dma_start(
+            out=w1_raw[:].rearrange("p g (u e) o -> p (g u) (e o)", e=PAIR),
+            in_=lin3_W1.rearrange("(gu p e) o -> p gu (e o)", p=P, e=PAIR),
+        )
+        for nt in range(NODE_TILES):
+            nc.sync.dma_start(out=hv_raw[:, nt, :], in_=h2[nt * P : (nt + 1) * P, H_SCAL:])
+        for nt in range(NODE_TILES):
+            nc.sync.dma_start(out=fs_raw[:, nt, :], in_=features[nt * P : (nt + 1) * P, :F_SCAL])
+        nc.sync.dma_start(
+            out=b0[:].rearrange("p b e c -> p b (e c)"),
+            in_=byp_W0.rearrange("(b p e) c -> p b (e c)", p=P, e=PAIR),
+        )
+        for nt in range(NODE_TILES):
+            nc.sync.dma_start(out=hs_raw[:, nt, :], in_=h2[nt * P : (nt + 1) * P, :H_SCAL])
+        for g in range(S_PASSES):
+            nc.sync.dma_start(
+                out=w0_raw[:, g].rearrange("p (u e) c -> p u (e c)", e=PAIR),
+                in_=lin3_W0[g * K_PASS : (g + 1) * K_PASS, :].rearrange("(u p e) c -> p u (e c)", p=P, e=PAIR),
+            )
+
+        f_t = keep.tile([P, FS_UNITS + DV * FV_BLOCKS, NODES, PAIR], BF16)
+
+        def features_units(first_unit, words_of_unit):
+            bank = psum_in.tile([P, 2, NODES], F32, tag="bank_in")
+            for slot in range(2):
+                transpose_words(nc, bank, slot, words_of_unit(first_unit + slot), ident)
+            nc.scalar.copy(
+                out=f_t[:, first_unit : first_unit + 2].rearrange("p s n e -> p (s n e)"),
+                in_=bank[:].rearrange("p s n -> p (s n)").bitcast(BF16),
+            )
+
+        def vector_words(unit):
+            b, r = divmod(unit - FS_UNITS, DV)
+            first = DV * P * b + r
+            return lambda nt: fv_raw[:, nt, :].bitcast(F32)[:, first : first + DV * (P - 1) + 1 : DV]
+
+        def scalar_words(unit):
+            return lambda nt: fs_raw[:, nt, :].bitcast(F32)[:, unit * P : (unit + 1) * P]
+
+        for first_unit in range(FS_UNITS, FS_UNITS + DV * FV_BLOCKS, 2):
+            features_units(first_unit, vector_words)
+
+        w1_codes = keep.tile([P, V_PASSES, O_VEC], U32, align_bytes=64)
+        w1_scales = keep.tile([P, V_PASSES, O_VEC], U8, align_bytes=64)
+        for g in range(V_PASSES):
+            quantise_weight_pass(nc, stage, w1_raw[:, g], w1_codes[:, g, :], w1_scales[:, g, :])
+
+        y_v = keep.tile([P, V_TILES, DV, NODES], F32)
+        for ct in range(V_TILES):
+            chans = slice(ct * P, (ct + 1) * P)
+            acc01 = psum_acc.tile([P, 2, NODES], F32, tag="acc")
+            acc2 = psum_acc.tile([P, 1, NODES], F32, tag="acc")
+            for d in range(DV):
+                acc = acc01[:, d, :] if d < 2 else acc2[:, 0, :]
+                for b in range(FV_BLOCKS):
+                    for e in range(PAIR):
+                        r, half = divmod(DV * e + d, PAIR)
+                        nc.tensor.matmul(
+                            out=acc,
+                            lhsT=b1[:, b, e, chans],
+                            rhs=f_t[:, FS_UNITS + DV * b + r, :, half],
+                            start=(b == 0 and e == 0),
+                            stop=(b == FV_BLOCKS - 1 and e == PAIR - 1),
+                        )
+            nc.scalar.activation(out=y_v[:, ct, 0:2, :], in_=acc01[:], func=ACT.Copy, scale=F_VEC**-0.5)
+            nc.scalar.activation(out=y_v[:, ct, 2:3, :], in_=acc2[:], func=ACT.Copy, scale=F_VEC**-0.5)
+
+        H_UNITS = S_PASSES + DV * V_PASSES
+        h_codes = keep.tile([P, H_UNITS, NODES], U32, align_bytes=64)
+        h_scales = keep.tile([P, H_UNITS, NODES], U8, align_bytes=64)
+
+        def quantise_h2_unit(unit, words_of_half):
+            bank = psum_in.tile([P, 2, NODES], F32, tag="bank_in")
+            for u in range(2):
+                transpose_words(nc, bank, u, words_of_half(u), ident)
+            grouped = stage.tile([P, NODES * PACK], BF16, align_bytes=64, tag="h_grouped", bufs=3)
+            nc.scalar.copy(
+                out=grouped[:].bitcast(F32).rearrange("p (n u) -> p n u", u=2),
+                in_=bank[:].rearrange("p u n -> p n u"),
+            )
+            nc.vector.quantize_mx(
+                out=h_codes[:, unit, :].bitcast(FP8X4), scales=h_scales[:, unit, :], in_=grouped[:]
+            )
+
+        hv_sorted = keep.tile([P, NODE_TILES, DV, H_VEC], BF16)
+        for nt in range(NODE_TILES):
+            nc.vector.tensor_copy(out=hv_sorted[:, nt], in_=hv_raw[:, nt, :].rearrange("p (i d) -> p d i", d=DV))
+
+        def h2_vector_words(g, d):
+            def words_of_half(u):
+                first = (PAIR * g + u) * P
+                return lambda nt: hv_sorted[:, nt, d, :].bitcast(F32)[:, first : first + P]
+
+            return words_of_half
+
+        def h2_scalar_words(g):
+            def words_of_half(u):
+                first = (PAIR * g + u) * P
+                return lambda nt: hs_raw[:, nt, :].bitcast(F32)[:, first : first + P]
+
+            return words_of_half
+
+        for g in range(V_PASSES):
+            for d in range(DV):
+                quantise_h2_unit(S_PASSES + DV * g + d, h2_vector_words(g, d))
+
+        for first_unit in range(0, FS_UNITS, 2):
+            features_units(first_unit, scalar_words)
+
+        bn_rows_f32 = const.tile([P, P], F32)
+        nc.vector.tensor_copy(out=bn_rows_f32[:], in_=bn_rows[:])
+        bn_bank = psum_in.tile([P, P], F32, tag="bank_in")
+        nc.tensor.transpose(bn_bank[:], bn_rows_f32[:], ident[:])
+        bn_cols = const.tile([P, W_ROWS + B_ROWS], F32)
+        nc.vector.tensor_copy(out=bn_cols[:], in_=bn_bank[:, : W_ROWS + B_ROWS])
+        weight_s = bn_cols[:, 0:S_TILES]
+        weight_v = bn_cols[:, S_TILES:W_ROWS]
+        bias_s = bn_cols[:, W_ROWS : W_ROWS + B_ROWS]
+
+        out_v = keep.tile([P, NODE_TILES, DV * O_VEC], F32)
+        sumsq_v = small.tile([P, V_TILES], F32)
+        std_v = small.tile([P, V_TILES], F32)
+        rstd_v = small.tile([P, V_TILES], F32)
+        gain_v = small.tile([P, V_TILES], F32)
+        for ct in range(V_TILES):
+            chans = slice(ct * P, (ct + 1) * P)
+            one = slice(ct, ct + 1)
+            acc01 = psum_acc.tile([P, 2, NODES], F32, tag="acc")
+            acc2 = psum_acc.tile([P, 1, NODES], F32, tag="acc")
+            for acc, first_d, n_d in ((acc01, 0, 2), (acc2, 2, 1)):
+                for g in range(V_PASSES):
+                    units = slice(S_PASSES + DV * g + first_d, S_PASSES + DV * g + first_d + n_d)
+                    nc.tensor.matmul_mx(
+                        out=acc[:].rearrange("p d n -> p (d n)"),
+                        lhsT=w1_codes[:, g, chans].bitcast(FP8X4),
+                        lhsT_scale=w1_scales[:, g, chans],
+                        rhs=h_codes[:, units, :].rearrange("p d n -> p (d n)").bitcast(FP8X4),
+                        rhs_scale=h_scales[:, units, :].rearrange("p d n -> p (d n)"),
+                        start=(g == 0),
+                        stop=(g == V_PASSES - 1),
+                    )
+                part = y_v[:, ct, first_d : first_d + n_d, :]
+                nc.vector.scalar_tensor_tensor(
+                    out=part, in0=acc[:], scalar=H_VEC**-0.5, in1=part, op0=ALU.mult, op1=ALU.add
+                )
+            squares = stage.tile([P, DV, NODES], BF16, tag="squares")
+            nc.scalar.activation(out=squares[:], in_=y_v[:, ct], func=ACT.Square, accum_out=sumsq_v[:, one])
+            nc.scalar.activation(
+                out=std_v[:, one], in_=sumsq_v[:, one], func=ACT.Sqrt, scale=1.0 / (DV * NODES), bias=eps[:]
+            )
+            nc.vector.reciprocal(out=rstd_v[:, one], in_=std_v[:, one])
+            nc.vector.tensor_mul(out=gain_v[:, one], in0=rstd_v[:, one], in1=weight_v[:, one])
+            nc.vector.tensor_scalar_mul(out=y_v[:, ct], in0=y_v[:, ct], scalar1=gain_v[:, one])
+            for nt in range(NODE_TILES):
+                back = psum_back.tile([P, DV, P], F32, tag="back")
+                for d in range(DV):
+                    nc.tensor.transpose(back[:, d, :], y_v[:, ct, d, nt * P : (nt + 1) * P], ident[:])
+                nc.scalar.copy(
+                    out=out_v[:, nt, DV * P * ct : DV * P * (ct + 1)].rearrange("p (o d) -> p o d", d=DV),
+                    in_=back[:].rearrange("p d o -> p o d"),
+                )
+
+        y_s = keep.tile([P, S_TILES, NODES], F32)
+        for pair in range(S_TILES // 2):
+            acc = psum_acc.tile([P, 2, NODES], F32, tag="acc")
+            for j in range(2):
+                ct = 2 * pair + j
+                for b in range(FS_UNITS):
+                    for e in range(PAIR):
+                        nc.tensor.matmul(
+                            out=acc[:, j, :],
+                            lhsT=b0[:, b, e, ct * P : (ct + 1) * P],
+                            rhs=f_t[:, b, :, e],
+                            start=(b == 0 and e == 0),
+                            stop=(b == FS_UNITS - 1 and e == PAIR - 1),
+                        )
+            nc.scalar.activation(out=y_s[:, 2 * pair : 2 * pair + 2, :], in_=acc[:], func=ACT.Copy, scale=F_SCAL**-0.5)
+
+        for g in range(S_PASSES):
+            quantise_h2_unit(g, h2_scalar_words(g))
+        w0_codes = keep.tile([P, S_PASSES, O_SCAL], U32, align_bytes=64)
+        w0_scales = keep.tile([P, S_PASSES, O_SCAL], U8, align_bytes=64)
+        for g in range(S_PASSES):
+            quantise_weight_pass(nc, stage, w0_raw[:, g], w0_codes[:, g, :], w0_scales[:, g, :])
+
+        out_s = keep.tile([P, NODE_TILES, O_SCAL], F32)
+        sum_s = small.tile([P, S_TILES], F32)
+        negmean_s = small.tile([P, S_TILES], F32)
+        sumsq_s = small.tile([P, S_TILES], F32)
+        std_s = small.tile([P, S_TILES], F32)
+        rstd_s = small.tile([P, S_TILES], F32)
+        gain_s = small.tile([P, S_TILES], F32)
+        shift_s = small.tile([P, S_TILES], F32)
+        out_by_tile = out.rearrange("(nt p) c -> p nt c", p=P)
+        for nt in range(NODE_TILES):
+            nc.sync.dma_start(out=out[nt * P : (nt + 1) * P, O_SCAL:], in_=out_v[:, nt, :])
+        for pair in range(S_TILES // 2):
+            two = slice(2 * pair, 2 * pair + 2)
+            acc = psum_acc.tile([P, 2, NODES], F32, tag="acc")
+            for j in range(2):
+                ct = 2 * pair + j
+                chans = slice(ct * P, (ct + 1) * P)
+                for g in range(S_PASSES):
+                    nc.tensor.matmul_mx(
+                        out=acc[:, j, :],
+                        lhsT=w0_codes[:, g, chans].bitcast(FP8X4),
+                        lhsT_scale=w0_scales[:, g, chans],
+                        rhs=h_codes[:, g, :].bitcast(FP8X4),
+                        rhs_scale=h_scales[:, g, :],
+                        start=(g == 0),
+                        stop=(g == S_PASSES - 1),
+                    )
+                nc.vector.scalar_tensor_tensor(
+                    out=y_s[:, ct, :],
+                    in0=acc[:, j, :],
+                    scalar=H_SCAL**-0.5,
+                    in1=y_s[:, ct, :],
+                    op0=ALU.mult,
+                    op1=ALU.add,
+                    accum_out=sum_s[:, ct : ct + 1],
+                )
+            nc.vector.tensor_scalar_mul(out=negmean_s[:, two], in0=sum_s[:, two], scalar1=-1.0 / NODES)
+            for ct in (2 * pair, 2 * pair + 1):
+                squares = stage.tile([P, NODES], BF16, tag="squares")
+                nc.scalar.activation(
+                    out=squares[:],
+                    in_=y_s[:, ct, :],
+                    func=ACT.Square,
+                    bias=negmean_s[:, ct : ct + 1],
+                    accum_out=sumsq_s[:, ct : ct + 1],
+                )
+            nc.scalar.activation(out=std_s[:, two], in_=sumsq_s[:, two], func=ACT.Sqrt, scale=1.0 / NODES, bias=eps[:])
+            nc.vector.reciprocal(out=rstd_s[:, two], in_=std_s[:, two])
+            nc.vector.tensor_mul(out=gain_s[:, two], in0=rstd_s[:, two], in1=weight_s[:, two])
+            nc.vector.tensor_mul(out=shift_s[:, two], in0=negmean_s[:, two], in1=gain_s[:, two])
+            nc.vector.tensor_add(out=shift_s[:, two], in0=shift_s[:, two], in1=bias_s[:, two])
+            back = psum_back.tile([P, NODE_TILES, 2, P], F32, tag="back")
+            for j in range(2):
+                ct = 2 * pair + j
+                nc.vector.tensor_scalar(
+                    out=y_s[:, ct, :],
+                    in0=y_s[:, ct, :],
+                    scalar1=gain_s[:, ct : ct + 1],
+                    scalar2=shift_s[:, ct : ct + 1],
+                    op0=ALU.mult,
+                    op1=ALU.add,
+                )
+                for nt in range(NODE_TILES):
+                    nc.tensor.transpose(back[:, nt, j, :], y_s[:, ct, nt * P : (nt + 1) * P], ident[:])
+            cols = slice(2 * pair * P, (2 * pair + 2) * P)
+            nc.scalar.copy(out=out_s[:, :, cols], in_=back[:].rearrange("p nt j c -> p nt (j c)"))
+            nc.sync.dma_start(out=out_by_tile[:, :, cols], in_=out_s[:, :, cols])

@@ -31,29 +31,31 @@ S_TILES = O_SCAL // P
 V_TILES = O_VEC // P
 FS_UNITS = F_SCAL // K_WORDS
 FV_BLOCKS = F_VEC // K_WORDS
+H_UNITS = S_PASSES + DV * V_PASSES
+QUAD = 4
 
 SCALAR_SHARE = 4
 
 FLOPS = 2 * NODES * (H_SCAL + F_SCAL) * O_SCAL + 2 * NODES * DV * (H_VEC + F_VEC) * O_VEC
 
 
-def quantise_weight_pass(nc, stage, raw, codes, scales):
+def regroup_weight_pass(nc, stage, raw):
     width = raw.shape[2]
     grouped = stage.tile([P, width, PACK], BF16, align_bytes=64, tag="w_grouped")
     split = width - width // SCALAR_SHARE
-    nc.vector.tensor_copy(
-        out=grouped[:, :split, :].rearrange("p (c i) t -> p c t i", i=4),
-        in_=raw[:, :, :split].rearrange("p t (c i) -> p c t i", i=4),
-    )
     nc.scalar.copy(
         out=grouped[:, split:, :].rearrange("p (c i) t -> p c t i", i=4),
         in_=raw[:, :, split:].rearrange("p t (c i) -> p c t i", i=4),
     )
-    nc.vector.quantize_mx(
-        out=codes.bitcast(FP8X4),
-        scales=scales,
-        in_=grouped[:].rearrange("p c t -> p (c t)"),
+    nc.vector.tensor_copy(
+        out=grouped[:, :split, :].rearrange("p (c i) t -> p c t i", i=4),
+        in_=raw[:, :, :split].rearrange("p t (c i) -> p c t i", i=4),
     )
+    return grouped
+
+
+def quantise(nc, grouped, codes, scales):
+    nc.vector.quantize_mx(out=codes.bitcast(FP8X4), scales=scales, in_=grouped)
 
 
 def transpose_words(nc, bank, slot, words_of_tile, ident):
@@ -66,13 +68,13 @@ def tile_feedforward_pb_kernel(
 ):
     nc = tc.nc
     with ExitStack() as ctx:
+        ctx.enter_context(tc.manual_schedule())
         const = ctx.enter_context(tc.tile_pool(name="const", bufs=1))
         keep = ctx.enter_context(tc.tile_pool(name="keep", bufs=1))
         stage = ctx.enter_context(tc.tile_pool(name="stage", bufs=2))
         small = ctx.enter_context(tc.tile_pool(name="small", bufs=1))
-        psum_in = ctx.enter_context(tc.psum_pool(name="psum_in", bufs=2))
+        psum_t = ctx.enter_context(tc.psum_pool(name="psum_t", bufs=4))
         psum_acc = ctx.enter_context(tc.psum_pool(name="psum_acc", bufs=4))
-        psum_back = ctx.enter_context(tc.psum_pool(name="psum_back", bufs=2))
 
         ident = const.tile([P, P], F32)
         make_identity(nc, ident[:])
@@ -90,6 +92,23 @@ def tile_feedforward_pb_kernel(
         w1_raw = keep.tile([P, V_PASSES, PACK, O_VEC], BF16)
         w0_raw = keep.tile([P, S_PASSES, PACK, O_SCAL], BF16)
 
+        def load_node_tiles(tile, columns):
+            for nt in range(NODE_TILES):
+                nc.sync.dma_start(out=tile[:, nt, :], in_=columns[nt * P : (nt + 1) * P, :])
+
+        def load_mx_weight(tile, weight, passes):
+            for g in range(passes):
+                nc.sync.dma_start(
+                    out=tile[:, g].rearrange("p (u e) c -> p u (e c)", e=PAIR),
+                    in_=weight[g * K_PASS : (g + 1) * K_PASS, :].rearrange("(u p e) c -> p u (e c)", p=P, e=PAIR),
+                )
+
+        def load_plain_weight(tile, weight):
+            nc.sync.dma_start(
+                out=tile[:].rearrange("p b e c -> p b (e c)"),
+                in_=weight.rearrange("(b p e) c -> p b (e c)", p=P, e=PAIR),
+            )
+
         W_ROWS = (O_SCAL + O_VEC) // P
         B_ROWS = O_SCAL // P
         bn_rows = const.tile([P, P], BF16)
@@ -97,36 +116,19 @@ def tile_feedforward_pb_kernel(
         nc.sync.dma_start(out=bn_rows[0:W_ROWS, :], in_=bn_weight.rearrange("(r c) -> r c", c=P))
         nc.sync.dma_start(out=bn_rows[W_ROWS : W_ROWS + B_ROWS, :], in_=bn_bias.rearrange("(r c) -> r c", c=P))
 
-        for nt in range(NODE_TILES):
-            nc.sync.dma_start(out=fv_raw[:, nt, :], in_=features[nt * P : (nt + 1) * P, F_SCAL:])
-        nc.sync.dma_start(
-            out=b1[:].rearrange("p b e o -> p b (e o)"),
-            in_=byp_W1.rearrange("(b p e) o -> p b (e o)", p=P, e=PAIR),
-        )
-        nc.sync.dma_start(
-            out=w1_raw[:].rearrange("p g (u e) o -> p (g u) (e o)", e=PAIR),
-            in_=lin3_W1.rearrange("(gu p e) o -> p gu (e o)", p=P, e=PAIR),
-        )
-        for nt in range(NODE_TILES):
-            nc.sync.dma_start(out=hv_raw[:, nt, :], in_=h2[nt * P : (nt + 1) * P, H_SCAL:])
-        for nt in range(NODE_TILES):
-            nc.sync.dma_start(out=fs_raw[:, nt, :], in_=features[nt * P : (nt + 1) * P, :F_SCAL])
-        nc.sync.dma_start(
-            out=b0[:].rearrange("p b e c -> p b (e c)"),
-            in_=byp_W0.rearrange("(b p e) c -> p b (e c)", p=P, e=PAIR),
-        )
-        for nt in range(NODE_TILES):
-            nc.sync.dma_start(out=hs_raw[:, nt, :], in_=h2[nt * P : (nt + 1) * P, :H_SCAL])
-        for g in range(S_PASSES):
-            nc.sync.dma_start(
-                out=w0_raw[:, g].rearrange("p (u e) c -> p u (e c)", e=PAIR),
-                in_=lin3_W0[g * K_PASS : (g + 1) * K_PASS, :].rearrange("(u p e) c -> p u (e c)", p=P, e=PAIR),
-            )
+        load_node_tiles(fv_raw, features[:, F_SCAL:])
+        load_plain_weight(b1, byp_W1)
+        load_mx_weight(w1_raw, lin3_W1, V_PASSES)
+        load_node_tiles(hv_raw, h2[:, H_SCAL:])
+        load_node_tiles(hs_raw, h2[:, :H_SCAL])
+        load_node_tiles(fs_raw, features[:, :F_SCAL])
+        load_plain_weight(b0, byp_W0)
+        load_mx_weight(w0_raw, lin3_W0, S_PASSES)
 
         f_t = keep.tile([P, FS_UNITS + DV * FV_BLOCKS, NODES, PAIR], BF16)
 
         def features_units(first_unit, words_of_unit):
-            bank = psum_in.tile([P, 2, NODES], F32, tag="bank_in")
+            bank = psum_t.tile([P, 2, NODES], F32, tag="t")
             for slot in range(2):
                 transpose_words(nc, bank, slot, words_of_unit(first_unit + slot), ident)
             nc.scalar.copy(
@@ -147,8 +149,9 @@ def tile_feedforward_pb_kernel(
 
         w1_codes = keep.tile([P, V_PASSES, O_VEC], U32, align_bytes=64)
         w1_scales = keep.tile([P, V_PASSES, O_VEC], U8, align_bytes=64)
+        w1_grouped = [regroup_weight_pass(nc, stage, w1_raw[:, g]) for g in range(V_PASSES)]
         for g in range(V_PASSES):
-            quantise_weight_pass(nc, stage, w1_raw[:, g], w1_codes[:, g, :], w1_scales[:, g, :])
+            quantise(nc, w1_grouped[g][:].rearrange("p c t -> p (c t)"), w1_codes[:, g, :], w1_scales[:, g, :])
 
         y_v = keep.tile([P, V_TILES, DV, NODES], F32)
         for ct in range(V_TILES):
@@ -170,22 +173,22 @@ def tile_feedforward_pb_kernel(
             nc.scalar.activation(out=y_v[:, ct, 0:2, :], in_=acc01[:], func=ACT.Copy, scale=F_VEC**-0.5)
             nc.scalar.activation(out=y_v[:, ct, 2:3, :], in_=acc2[:], func=ACT.Copy, scale=F_VEC**-0.5)
 
-        H_UNITS = S_PASSES + DV * V_PASSES
         h_codes = keep.tile([P, H_UNITS, NODES], U32, align_bytes=64)
         h_scales = keep.tile([P, H_UNITS, NODES], U8, align_bytes=64)
 
-        def quantise_h2_unit(unit, words_of_half):
-            bank = psum_in.tile([P, 2, NODES], F32, tag="bank_in")
+        def transpose_h2_unit(words_of_half):
+            bank = psum_t.tile([P, 2, NODES], F32, tag="t")
             for u in range(2):
                 transpose_words(nc, bank, u, words_of_half(u), ident)
-            grouped = stage.tile([P, NODES * PACK], BF16, align_bytes=64, tag="h_grouped", bufs=3)
+            grouped = stage.tile([P, NODES * PACK], BF16, align_bytes=64, tag="h_grouped", bufs=4)
             nc.scalar.copy(
                 out=grouped[:].bitcast(F32).rearrange("p (n u) -> p n u", u=2),
                 in_=bank[:].rearrange("p u n -> p n u"),
             )
-            nc.vector.quantize_mx(
-                out=h_codes[:, unit, :].bitcast(FP8X4), scales=h_scales[:, unit, :], in_=grouped[:]
-            )
+            return grouped
+
+        def quantise_h2_unit(unit, grouped):
+            quantise(nc, grouped[:], h_codes[:, unit, :], h_scales[:, unit, :])
 
         hv_sorted = keep.tile([P, NODE_TILES, DV, H_VEC], BF16)
         for nt in range(NODE_TILES):
@@ -205,16 +208,18 @@ def tile_feedforward_pb_kernel(
 
             return words_of_half
 
+        waiting = None
         for g in range(V_PASSES):
             for d in range(DV):
-                quantise_h2_unit(S_PASSES + DV * g + d, h2_vector_words(g, d))
-
-        for first_unit in range(0, FS_UNITS, 2):
-            features_units(first_unit, scalar_words)
+                grouped = transpose_h2_unit(h2_vector_words(g, d))
+                if waiting is not None:
+                    quantise_h2_unit(*waiting)
+                waiting = (S_PASSES + DV * g + d, grouped)
+        quantise_h2_unit(*waiting)
 
         bn_rows_f32 = const.tile([P, P], F32)
         nc.vector.tensor_copy(out=bn_rows_f32[:], in_=bn_rows[:])
-        bn_bank = psum_in.tile([P, P], F32, tag="bank_in")
+        bn_bank = psum_t.tile([P, P], F32, tag="t")
         nc.tensor.transpose(bn_bank[:], bn_rows_f32[:], ident[:])
         bn_cols = const.tile([P, W_ROWS + B_ROWS], F32)
         nc.vector.tensor_copy(out=bn_cols[:], in_=bn_bank[:, : W_ROWS + B_ROWS])
@@ -222,14 +227,16 @@ def tile_feedforward_pb_kernel(
         weight_v = bn_cols[:, S_TILES:W_ROWS]
         bias_s = bn_cols[:, W_ROWS : W_ROWS + B_ROWS]
 
-        out_v = keep.tile([P, NODE_TILES, DV * O_VEC], F32)
+        hs_grouped = [transpose_h2_unit(h2_scalar_words(g)) for g in range(S_PASSES)]
+        for first_unit in range(0, FS_UNITS, 2):
+            features_units(first_unit, scalar_words)
+
         sumsq_v = small.tile([P, V_TILES], F32)
         std_v = small.tile([P, V_TILES], F32)
         rstd_v = small.tile([P, V_TILES], F32)
         gain_v = small.tile([P, V_TILES], F32)
         for ct in range(V_TILES):
             chans = slice(ct * P, (ct + 1) * P)
-            one = slice(ct, ct + 1)
             acc01 = psum_acc.tile([P, 2, NODES], F32, tag="acc")
             acc2 = psum_acc.tile([P, 1, NODES], F32, tag="acc")
             for acc, first_d, n_d in ((acc01, 0, 2), (acc2, 2, 1)):
@@ -248,28 +255,30 @@ def tile_feedforward_pb_kernel(
                 nc.vector.scalar_tensor_tensor(
                     out=part, in0=acc[:], scalar=H_VEC**-0.5, in1=part, op0=ALU.mult, op1=ALU.add
                 )
-            squares = stage.tile([P, DV, NODES], BF16, tag="squares")
-            nc.scalar.activation(out=squares[:], in_=y_v[:, ct], func=ACT.Square, accum_out=sumsq_v[:, one])
+            squares = stage.tile([P, DV, NODES], BF16, tag="squares", bufs=4)
             nc.scalar.activation(
-                out=std_v[:, one], in_=sumsq_v[:, one], func=ACT.Sqrt, scale=1.0 / (DV * NODES), bias=eps[:]
+                out=squares[:], in_=y_v[:, ct], func=ACT.Square, accum_out=sumsq_v[:, ct : ct + 1]
             )
-            nc.vector.reciprocal(out=rstd_v[:, one], in_=std_v[:, one])
-            nc.vector.tensor_mul(out=gain_v[:, one], in0=rstd_v[:, one], in1=weight_v[:, one])
-            nc.vector.tensor_scalar_mul(out=y_v[:, ct], in0=y_v[:, ct], scalar1=gain_v[:, one])
-            for nt in range(NODE_TILES):
-                back = psum_back.tile([P, DV, P], F32, tag="back")
-                for d in range(DV):
-                    nc.tensor.transpose(back[:, d, :], y_v[:, ct, d, nt * P : (nt + 1) * P], ident[:])
-                nc.scalar.copy(
-                    out=out_v[:, nt, DV * P * ct : DV * P * (ct + 1)].rearrange("p (o d) -> p o d", d=DV),
-                    in_=back[:].rearrange("p d o -> p o d"),
-                )
 
+        for g in range(S_PASSES):
+            quantise_h2_unit(g, hs_grouped[g])
+
+        w0_codes = keep.tile([P, S_PASSES, O_SCAL], U32, align_bytes=64)
+        w0_scales = keep.tile([P, S_PASSES, O_SCAL], U8, align_bytes=64)
+        w0_grouped = regroup_weight_pass(nc, stage, w0_raw[:, 0])
+
+        nc.scalar.activation(out=std_v[:], in_=sumsq_v[:], func=ACT.Sqrt, scale=1.0 / (DV * NODES), bias=eps[:])
+        nc.vector.reciprocal(out=rstd_v[:], in_=std_v[:])
+        nc.vector.tensor_mul(out=gain_v[:], in0=rstd_v[:], in1=weight_v)
+
+        out_v = keep.tile([P, NODE_TILES, DV * O_VEC], F32)
         y_s = keep.tile([P, S_TILES, NODES], F32)
-        for pair in range(S_TILES // 2):
+        assert V_TILES == S_PASSES == S_TILES // 2
+        for i in range(V_TILES):
+            nc.vector.tensor_scalar_mul(out=y_v[:, i], in0=y_v[:, i], scalar1=gain_v[:, i : i + 1])
             acc = psum_acc.tile([P, 2, NODES], F32, tag="acc")
             for j in range(2):
-                ct = 2 * pair + j
+                ct = 2 * i + j
                 for b in range(FS_UNITS):
                     for e in range(PAIR):
                         nc.tensor.matmul(
@@ -279,32 +288,36 @@ def tile_feedforward_pb_kernel(
                             start=(b == 0 and e == 0),
                             stop=(b == FS_UNITS - 1 and e == PAIR - 1),
                         )
-            nc.scalar.activation(out=y_s[:, 2 * pair : 2 * pair + 2, :], in_=acc[:], func=ACT.Copy, scale=F_SCAL**-0.5)
-
-        for g in range(S_PASSES):
-            quantise_h2_unit(g, h2_scalar_words(g))
-        w0_codes = keep.tile([P, S_PASSES, O_SCAL], U32, align_bytes=64)
-        w0_scales = keep.tile([P, S_PASSES, O_SCAL], U8, align_bytes=64)
-        for g in range(S_PASSES):
-            quantise_weight_pass(nc, stage, w0_raw[:, g], w0_codes[:, g, :], w0_scales[:, g, :])
+            nc.scalar.activation(out=y_s[:, 2 * i : 2 * i + 2, :], in_=acc[:], func=ACT.Copy, scale=F_SCAL**-0.5)
+            quantise(nc, w0_grouped[:].rearrange("p c t -> p (c t)"), w0_codes[:, i, :], w0_scales[:, i, :])
+            if i + 1 < S_PASSES:
+                w0_grouped = regroup_weight_pass(nc, stage, w0_raw[:, i + 1])
+            for nt in range(NODE_TILES):
+                back = psum_t.tile([P, DV, P], F32, tag="t")
+                for d in range(DV):
+                    nc.tensor.transpose(back[:, d, :], y_v[:, i, d, nt * P : (nt + 1) * P], ident[:])
+                nc.scalar.copy(
+                    out=out_v[:, nt, DV * P * i : DV * P * (i + 1)].rearrange("p (o d) -> p o d", d=DV),
+                    in_=back[:].rearrange("p d o -> p o d"),
+                )
+        for nt in range(NODE_TILES):
+            nc.sync.dma_start(out=out[nt * P : (nt + 1) * P, O_SCAL:], in_=out_v[:, nt, :])
 
         out_s = keep.tile([P, NODE_TILES, O_SCAL], F32)
         sum_s = small.tile([P, S_TILES], F32)
-        negmean_s = small.tile([P, S_TILES], F32)
         sumsq_s = small.tile([P, S_TILES], F32)
+        negmean_s = small.tile([P, S_TILES], F32)
+        offset_s = small.tile([P, S_TILES], F32)
+        var_s = small.tile([P, S_TILES], F32)
         std_s = small.tile([P, S_TILES], F32)
         rstd_s = small.tile([P, S_TILES], F32)
         gain_s = small.tile([P, S_TILES], F32)
         shift_s = small.tile([P, S_TILES], F32)
         out_by_tile = out.rearrange("(nt p) c -> p nt c", p=P)
-        for nt in range(NODE_TILES):
-            nc.sync.dma_start(out=out[nt * P : (nt + 1) * P, O_SCAL:], in_=out_v[:, nt, :])
-        for pair in range(S_TILES // 2):
-            two = slice(2 * pair, 2 * pair + 2)
+        for pair_ct in range(0, S_TILES, 2):
             acc = psum_acc.tile([P, 2, NODES], F32, tag="acc")
             for j in range(2):
-                ct = 2 * pair + j
-                chans = slice(ct * P, (ct + 1) * P)
+                chans = slice((pair_ct + j) * P, (pair_ct + j + 1) * P)
                 for g in range(S_PASSES):
                     nc.tensor.matmul_mx(
                         out=acc[:, j, :],
@@ -315,6 +328,8 @@ def tile_feedforward_pb_kernel(
                         start=(g == 0),
                         stop=(g == S_PASSES - 1),
                     )
+            for j in range(2):
+                ct = pair_ct + j
                 nc.vector.scalar_tensor_tensor(
                     out=y_s[:, ct, :],
                     in0=acc[:, j, :],
@@ -324,34 +339,47 @@ def tile_feedforward_pb_kernel(
                     op1=ALU.add,
                     accum_out=sum_s[:, ct : ct + 1],
                 )
-            nc.vector.tensor_scalar_mul(out=negmean_s[:, two], in0=sum_s[:, two], scalar1=-1.0 / NODES)
-            for ct in (2 * pair, 2 * pair + 1):
-                squares = stage.tile([P, NODES], BF16, tag="squares")
+                squares = stage.tile([P, NODES], BF16, tag="squares", bufs=4)
                 nc.scalar.activation(
                     out=squares[:],
                     in_=y_s[:, ct, :],
                     func=ACT.Square,
-                    bias=negmean_s[:, ct : ct + 1],
+                    scale=-1.0,
+                    bias=y_s[:, ct, 0:1],
                     accum_out=sumsq_s[:, ct : ct + 1],
                 )
-            nc.scalar.activation(out=std_s[:, two], in_=sumsq_s[:, two], func=ACT.Sqrt, scale=1.0 / NODES, bias=eps[:])
-            nc.vector.reciprocal(out=rstd_s[:, two], in_=std_s[:, two])
-            nc.vector.tensor_mul(out=gain_s[:, two], in0=rstd_s[:, two], in1=weight_s[:, two])
-            nc.vector.tensor_mul(out=shift_s[:, two], in0=negmean_s[:, two], in1=gain_s[:, two])
-            nc.vector.tensor_add(out=shift_s[:, two], in0=shift_s[:, two], in1=bias_s[:, two])
-            back = psum_back.tile([P, NODE_TILES, 2, P], F32, tag="back")
-            for j in range(2):
-                ct = 2 * pair + j
-                nc.vector.tensor_scalar(
-                    out=y_s[:, ct, :],
-                    in0=y_s[:, ct, :],
-                    scalar1=gain_s[:, ct : ct + 1],
-                    scalar2=shift_s[:, ct : ct + 1],
-                    op0=ALU.mult,
-                    op1=ALU.add,
-                )
-                for nt in range(NODE_TILES):
-                    nc.tensor.transpose(back[:, nt, j, :], y_s[:, ct, nt * P : (nt + 1) * P], ident[:])
-            cols = slice(2 * pair * P, (2 * pair + 2) * P)
-            nc.scalar.copy(out=out_s[:, :, cols], in_=back[:].rearrange("p nt j c -> p nt (j c)"))
-            nc.sync.dma_start(out=out_by_tile[:, :, cols], in_=out_s[:, :, cols])
+        for first_ct in range(0, S_TILES, QUAD):
+            quad = slice(first_ct, first_ct + QUAD)
+            nc.vector.tensor_scalar_mul(out=negmean_s[:, quad], in0=sum_s[:, quad], scalar1=-1.0 / NODES)
+            nc.vector.tensor_add(out=offset_s[:, quad], in0=y_s[:, quad, 0], in1=negmean_s[:, quad])
+            nc.vector.tensor_mul(out=offset_s[:, quad], in0=offset_s[:, quad], in1=offset_s[:, quad])
+            nc.vector.scalar_tensor_tensor(
+                out=var_s[:, quad],
+                in0=sumsq_s[:, quad],
+                scalar=1.0 / NODES,
+                in1=offset_s[:, quad],
+                op0=ALU.mult,
+                op1=ALU.subtract,
+            )
+            nc.scalar.activation(out=std_s[:, quad], in_=var_s[:, quad], func=ACT.Sqrt, bias=eps[:])
+            nc.vector.reciprocal(out=rstd_s[:, quad], in_=std_s[:, quad])
+            nc.vector.tensor_mul(out=gain_s[:, quad], in0=rstd_s[:, quad], in1=weight_s[:, quad])
+            nc.vector.tensor_mul(out=shift_s[:, quad], in0=negmean_s[:, quad], in1=gain_s[:, quad])
+            nc.vector.tensor_add(out=shift_s[:, quad], in0=shift_s[:, quad], in1=bias_s[:, quad])
+            for pair_ct in range(first_ct, first_ct + QUAD, 2):
+                back = psum_t.tile([P, NODE_TILES, 2, P], F32, tag="t")
+                for j in range(2):
+                    ct = pair_ct + j
+                    nc.vector.tensor_scalar(
+                        out=y_s[:, ct, :],
+                        in0=y_s[:, ct, :],
+                        scalar1=gain_s[:, ct : ct + 1],
+                        scalar2=shift_s[:, ct : ct + 1],
+                        op0=ALU.mult,
+                        op1=ALU.add,
+                    )
+                    for nt in range(NODE_TILES):
+                        nc.tensor.transpose(back[:, nt, j, :], y_s[:, ct, nt * P : (nt + 1) * P], ident[:])
+                cols = slice(pair_ct * P, (pair_ct + 2) * P)
+                nc.scalar.copy(out=out_s[:, :, cols], in_=back[:].rearrange("p nt j c -> p nt (j c)"))
+                nc.sync.dma_start(out=out_by_tile[:, :, cols], in_=out_s[:, :, cols])

@@ -68,7 +68,6 @@ def tile_feedforward_pb_kernel(
 ):
     nc = tc.nc
     with ExitStack() as ctx:
-        ctx.enter_context(tc.manual_schedule())
         const = ctx.enter_context(tc.tile_pool(name="const", bufs=1))
         keep = ctx.enter_context(tc.tile_pool(name="keep", bufs=1))
         stage = ctx.enter_context(tc.tile_pool(name="stage", bufs=2))
@@ -117,9 +116,9 @@ def tile_feedforward_pb_kernel(
         nc.sync.dma_start(out=bn_rows[W_ROWS : W_ROWS + B_ROWS, :], in_=bn_bias.rearrange("(r c) -> r c", c=P))
 
         load_node_tiles(fv_raw, features[:, F_SCAL:])
+        load_node_tiles(hv_raw, h2[:, H_SCAL:])
         load_plain_weight(b1, byp_W1)
         load_mx_weight(w1_raw, lin3_W1, V_PASSES)
-        load_node_tiles(hv_raw, h2[:, H_SCAL:])
         load_node_tiles(hs_raw, h2[:, :H_SCAL])
         load_node_tiles(fs_raw, features[:, :F_SCAL])
         load_plain_weight(b0, byp_W0)
@@ -146,32 +145,6 @@ def tile_feedforward_pb_kernel(
 
         for first_unit in range(FS_UNITS, FS_UNITS + DV * FV_BLOCKS, 2):
             features_units(first_unit, vector_words)
-
-        w1_codes = keep.tile([P, V_PASSES, O_VEC], U32, align_bytes=64)
-        w1_scales = keep.tile([P, V_PASSES, O_VEC], U8, align_bytes=64)
-        w1_grouped = [regroup_weight_pass(nc, stage, w1_raw[:, g]) for g in range(V_PASSES)]
-        for g in range(V_PASSES):
-            quantise(nc, w1_grouped[g][:].rearrange("p c t -> p (c t)"), w1_codes[:, g, :], w1_scales[:, g, :])
-
-        y_v = keep.tile([P, V_TILES, DV, NODES], F32)
-        for ct in range(V_TILES):
-            chans = slice(ct * P, (ct + 1) * P)
-            acc01 = psum_acc.tile([P, 2, NODES], F32, tag="acc")
-            acc2 = psum_acc.tile([P, 1, NODES], F32, tag="acc")
-            for d in range(DV):
-                acc = acc01[:, d, :] if d < 2 else acc2[:, 0, :]
-                for b in range(FV_BLOCKS):
-                    for e in range(PAIR):
-                        r, half = divmod(DV * e + d, PAIR)
-                        nc.tensor.matmul(
-                            out=acc,
-                            lhsT=b1[:, b, e, chans],
-                            rhs=f_t[:, FS_UNITS + DV * b + r, :, half],
-                            start=(b == 0 and e == 0),
-                            stop=(b == FV_BLOCKS - 1 and e == PAIR - 1),
-                        )
-            nc.scalar.activation(out=y_v[:, ct, 0:2, :], in_=acc01[:], func=ACT.Copy, scale=F_VEC**-0.5)
-            nc.scalar.activation(out=y_v[:, ct, 2:3, :], in_=acc2[:], func=ACT.Copy, scale=F_VEC**-0.5)
 
         h_codes = keep.tile([P, H_UNITS, NODES], U32, align_bytes=64)
         h_scales = keep.tile([P, H_UNITS, NODES], U8, align_bytes=64)
@@ -208,14 +181,35 @@ def tile_feedforward_pb_kernel(
 
             return words_of_half
 
-        waiting = None
+        w1_codes = keep.tile([P, V_PASSES, O_VEC], U32, align_bytes=64)
+        w1_scales = keep.tile([P, V_PASSES, O_VEC], U8, align_bytes=64)
+        for g in range(V_PASSES):
+            w1_grouped = regroup_weight_pass(nc, stage, w1_raw[:, g])
+            quantise(nc, w1_grouped[:].rearrange("p c t -> p (c t)"), w1_codes[:, g, :], w1_scales[:, g, :])
+
         for g in range(V_PASSES):
             for d in range(DV):
-                grouped = transpose_h2_unit(h2_vector_words(g, d))
-                if waiting is not None:
-                    quantise_h2_unit(*waiting)
-                waiting = (S_PASSES + DV * g + d, grouped)
-        quantise_h2_unit(*waiting)
+                quantise_h2_unit(S_PASSES + DV * g + d, transpose_h2_unit(h2_vector_words(g, d)))
+
+        y_v = keep.tile([P, V_TILES, DV, NODES], F32)
+        for ct in range(V_TILES):
+            chans = slice(ct * P, (ct + 1) * P)
+            acc01 = psum_acc.tile([P, 2, NODES], F32, tag="acc")
+            acc2 = psum_acc.tile([P, 1, NODES], F32, tag="acc")
+            for d in range(DV):
+                acc = acc01[:, d, :] if d < 2 else acc2[:, 0, :]
+                for b in range(FV_BLOCKS):
+                    for e in range(PAIR):
+                        r, half = divmod(DV * e + d, PAIR)
+                        nc.tensor.matmul(
+                            out=acc,
+                            lhsT=b1[:, b, e, chans],
+                            rhs=f_t[:, FS_UNITS + DV * b + r, :, half],
+                            start=(b == 0 and e == 0),
+                            stop=(b == FV_BLOCKS - 1 and e == PAIR - 1),
+                        )
+            nc.scalar.activation(out=y_v[:, ct, 0:2, :], in_=acc01[:], func=ACT.Copy, scale=F_VEC**-0.5)
+            nc.scalar.activation(out=y_v[:, ct, 2:3, :], in_=acc2[:], func=ACT.Copy, scale=F_VEC**-0.5)
 
         bn_rows_f32 = const.tile([P, P], F32)
         nc.vector.tensor_copy(out=bn_rows_f32[:], in_=bn_rows[:])
@@ -226,10 +220,6 @@ def tile_feedforward_pb_kernel(
         weight_s = bn_cols[:, 0:S_TILES]
         weight_v = bn_cols[:, S_TILES:W_ROWS]
         bias_s = bn_cols[:, W_ROWS : W_ROWS + B_ROWS]
-
-        hs_grouped = [transpose_h2_unit(h2_scalar_words(g)) for g in range(S_PASSES)]
-        for first_unit in range(0, FS_UNITS, 2):
-            features_units(first_unit, scalar_words)
 
         sumsq_v = small.tile([P, V_TILES], F32)
         std_v = small.tile([P, V_TILES], F32)
@@ -260,60 +250,54 @@ def tile_feedforward_pb_kernel(
                 out=squares[:], in_=y_v[:, ct], func=ACT.Square, accum_out=sumsq_v[:, ct : ct + 1]
             )
 
-        for g in range(S_PASSES):
-            quantise_h2_unit(g, hs_grouped[g])
-
-        w0_codes = keep.tile([P, S_PASSES, O_SCAL], U32, align_bytes=64)
-        w0_scales = keep.tile([P, S_PASSES, O_SCAL], U8, align_bytes=64)
-        w0_grouped = regroup_weight_pass(nc, stage, w0_raw[:, 0])
-
         nc.scalar.activation(out=std_v[:], in_=sumsq_v[:], func=ACT.Sqrt, scale=1.0 / (DV * NODES), bias=eps[:])
         nc.vector.reciprocal(out=rstd_v[:], in_=std_v[:])
         nc.vector.tensor_mul(out=gain_v[:], in0=rstd_v[:], in1=weight_v)
 
-        out_v = keep.tile([P, NODE_TILES, DV * O_VEC], F32)
+        for first_unit in range(0, FS_UNITS, 2):
+            features_units(first_unit, scalar_words)
+        for g in range(S_PASSES):
+            quantise_h2_unit(g, transpose_h2_unit(h2_scalar_words(g)))
+
+        w0_codes = keep.tile([P, S_PASSES, O_SCAL], U32, align_bytes=64)
+        w0_scales = keep.tile([P, S_PASSES, O_SCAL], U8, align_bytes=64)
+        for g in range(S_PASSES):
+            w0_grouped = regroup_weight_pass(nc, stage, w0_raw[:, g])
+            quantise(nc, w0_grouped[:].rearrange("p c t -> p (c t)"), w0_codes[:, g, :], w0_scales[:, g, :])
+
         y_s = keep.tile([P, S_TILES, NODES], F32)
-        assert V_TILES == S_PASSES == S_TILES // 2
-        for i in range(V_TILES):
-            nc.vector.tensor_scalar_mul(out=y_v[:, i], in0=y_v[:, i], scalar1=gain_v[:, i : i + 1])
+        for pair_ct in range(0, S_TILES, 2):
             acc = psum_acc.tile([P, 2, NODES], F32, tag="acc")
             for j in range(2):
-                ct = 2 * i + j
+                chans = slice((pair_ct + j) * P, (pair_ct + j + 1) * P)
                 for b in range(FS_UNITS):
                     for e in range(PAIR):
                         nc.tensor.matmul(
                             out=acc[:, j, :],
-                            lhsT=b0[:, b, e, ct * P : (ct + 1) * P],
+                            lhsT=b0[:, b, e, chans],
                             rhs=f_t[:, b, :, e],
                             start=(b == 0 and e == 0),
                             stop=(b == FS_UNITS - 1 and e == PAIR - 1),
                         )
-            nc.scalar.activation(out=y_s[:, 2 * i : 2 * i + 2, :], in_=acc[:], func=ACT.Copy, scale=F_SCAL**-0.5)
-            quantise(nc, w0_grouped[:].rearrange("p c t -> p (c t)"), w0_codes[:, i, :], w0_scales[:, i, :])
-            if i + 1 < S_PASSES:
-                w0_grouped = regroup_weight_pass(nc, stage, w0_raw[:, i + 1])
+            nc.scalar.activation(out=y_s[:, pair_ct : pair_ct + 2, :], in_=acc[:], func=ACT.Copy, scale=F_SCAL**-0.5)
+
+        out_v = keep.tile([P, NODE_TILES, DV * O_VEC], F32)
+        for ct in range(V_TILES):
+            nc.scalar.activation(out=y_v[:, ct], in_=y_v[:, ct], func=ACT.Copy, scale=gain_v[:, ct : ct + 1])
             for nt in range(NODE_TILES):
                 back = psum_t.tile([P, DV, P], F32, tag="t")
                 for d in range(DV):
-                    nc.tensor.transpose(back[:, d, :], y_v[:, i, d, nt * P : (nt + 1) * P], ident[:])
+                    nc.tensor.transpose(back[:, d, :], y_v[:, ct, d, nt * P : (nt + 1) * P], ident[:])
                 nc.scalar.copy(
-                    out=out_v[:, nt, DV * P * i : DV * P * (i + 1)].rearrange("p (o d) -> p o d", d=DV),
+                    out=out_v[:, nt, DV * P * ct : DV * P * (ct + 1)].rearrange("p (o d) -> p o d", d=DV),
                     in_=back[:].rearrange("p d o -> p o d"),
                 )
         for nt in range(NODE_TILES):
             nc.sync.dma_start(out=out[nt * P : (nt + 1) * P, O_SCAL:], in_=out_v[:, nt, :])
 
-        out_s = keep.tile([P, NODE_TILES, O_SCAL], F32)
-        sum_s = small.tile([P, S_TILES], F32)
-        sumsq_s = small.tile([P, S_TILES], F32)
-        negmean_s = small.tile([P, S_TILES], F32)
-        offset_s = small.tile([P, S_TILES], F32)
-        var_s = small.tile([P, S_TILES], F32)
-        std_s = small.tile([P, S_TILES], F32)
-        rstd_s = small.tile([P, S_TILES], F32)
-        gain_s = small.tile([P, S_TILES], F32)
-        shift_s = small.tile([P, S_TILES], F32)
-        out_by_tile = out.rearrange("(nt p) c -> p nt c", p=P)
+        BN_STATS = 6
+        stats_s = small.tile([P, S_TILES, BN_STATS], F32)
+        mean_var_s = small.tile([P, S_TILES, 2], F32)
         for pair_ct in range(0, S_TILES, 2):
             acc = psum_acc.tile([P, 2, NODES], F32, tag="acc")
             for j in range(2):
@@ -328,44 +312,27 @@ def tile_feedforward_pb_kernel(
                         start=(g == 0),
                         stop=(g == S_PASSES - 1),
                     )
-            for j in range(2):
-                ct = pair_ct + j
-                nc.vector.scalar_tensor_tensor(
-                    out=y_s[:, ct, :],
-                    in0=acc[:, j, :],
-                    scalar=H_SCAL**-0.5,
-                    in1=y_s[:, ct, :],
-                    op0=ALU.mult,
-                    op1=ALU.add,
-                    accum_out=sum_s[:, ct : ct + 1],
-                )
-                squares = stage.tile([P, NODES], BF16, tag="squares", bufs=4)
-                nc.scalar.activation(
-                    out=squares[:],
-                    in_=y_s[:, ct, :],
-                    func=ACT.Square,
-                    scale=-1.0,
-                    bias=y_s[:, ct, 0:1],
-                    accum_out=sumsq_s[:, ct : ct + 1],
-                )
+            pair = slice(pair_ct, pair_ct + 2)
+            nc.vector.scalar_tensor_tensor(
+                out=y_s[:, pair, :], in0=acc[:], scalar=H_SCAL**-0.5, in1=y_s[:, pair, :], op0=ALU.mult, op1=ALU.add
+            )
+            for ct in (pair_ct, pair_ct + 1):
+                nc.vector.bn_stats(out=stats_s[:, ct, :], in_=y_s[:, ct, :])
+                nc.vector.bn_aggr(out=mean_var_s[:, ct, :], in_=stats_s[:, ct, :])
+
+        out_s = keep.tile([P, NODE_TILES, O_SCAL], F32)
+        std_s = small.tile([P, S_TILES], F32)
+        rstd_s = small.tile([P, S_TILES], F32)
+        gain_s = small.tile([P, S_TILES], F32)
+        shift_s = small.tile([P, S_TILES], F32)
+        out_by_tile = out.rearrange("(nt p) c -> p nt c", p=P)
         for first_ct in range(0, S_TILES, QUAD):
             quad = slice(first_ct, first_ct + QUAD)
-            nc.vector.tensor_scalar_mul(out=negmean_s[:, quad], in0=sum_s[:, quad], scalar1=-1.0 / NODES)
-            nc.vector.tensor_add(out=offset_s[:, quad], in0=y_s[:, quad, 0], in1=negmean_s[:, quad])
-            nc.vector.tensor_mul(out=offset_s[:, quad], in0=offset_s[:, quad], in1=offset_s[:, quad])
-            nc.vector.scalar_tensor_tensor(
-                out=var_s[:, quad],
-                in0=sumsq_s[:, quad],
-                scalar=1.0 / NODES,
-                in1=offset_s[:, quad],
-                op0=ALU.mult,
-                op1=ALU.subtract,
-            )
-            nc.scalar.activation(out=std_s[:, quad], in_=var_s[:, quad], func=ACT.Sqrt, bias=eps[:])
+            nc.scalar.activation(out=std_s[:, quad], in_=mean_var_s[:, quad, 1], func=ACT.Sqrt, bias=eps[:])
             nc.vector.reciprocal(out=rstd_s[:, quad], in_=std_s[:, quad])
             nc.vector.tensor_mul(out=gain_s[:, quad], in0=rstd_s[:, quad], in1=weight_s[:, quad])
-            nc.vector.tensor_mul(out=shift_s[:, quad], in0=negmean_s[:, quad], in1=gain_s[:, quad])
-            nc.vector.tensor_add(out=shift_s[:, quad], in0=shift_s[:, quad], in1=bias_s[:, quad])
+            nc.vector.tensor_mul(out=shift_s[:, quad], in0=mean_var_s[:, quad, 0], in1=gain_s[:, quad])
+            nc.vector.tensor_sub(out=shift_s[:, quad], in0=bias_s[:, quad], in1=shift_s[:, quad])
             for pair_ct in range(first_ct, first_ct + QUAD, 2):
                 back = psum_t.tile([P, NODE_TILES, 2, P], F32, tag="t")
                 for j in range(2):

@@ -32,35 +32,23 @@ V_TILES = O_VEC // P
 FS_UNITS = F_SCAL // K_WORDS
 FV_BLOCKS = F_VEC // K_WORDS
 H_UNITS = S_PASSES + DV * V_PASSES
-QUAD = 4
-
-SCALAR_SHARE = 4
+HALF = 512
 
 FLOPS = 2 * NODES * (H_SCAL + F_SCAL) * O_SCAL + 2 * NODES * DV * (H_VEC + F_VEC) * O_VEC
 
-
-def regroup_weight_pass(nc, stage, raw):
-    width = raw.shape[2]
-    grouped = stage.tile([P, width, PACK], BF16, align_bytes=64, tag="w_grouped")
-    split = width - width // SCALAR_SHARE
-    nc.scalar.copy(
-        out=grouped[:, split:, :].rearrange("p (c i) t -> p c t i", i=4),
-        in_=raw[:, :, split:].rearrange("p t (c i) -> p c t i", i=4),
-    )
-    nc.vector.tensor_copy(
-        out=grouped[:, :split, :].rearrange("p (c i) t -> p c t i", i=4),
-        in_=raw[:, :, :split].rearrange("p t (c i) -> p c t i", i=4),
-    )
-    return grouped
+PIN = "none"
+SORT_ENGINES = ("v", "s", "g")
+S_COLS = 160
 
 
-def quantise(nc, grouped, codes, scales):
-    nc.vector.quantize_mx(out=codes.bitcast(FP8X4), scales=scales, in_=grouped)
-
-
-def transpose_words(nc, bank, slot, words_of_tile, ident):
-    for nt in range(NODE_TILES):
-        nc.tensor.transpose(bank[:, slot, nt * P : (nt + 1) * P], words_of_tile(nt), ident[:])
+def weave(a, b, na, nb):
+    steps, i, j = [], 0, 0
+    while i < len(a) or j < len(b):
+        steps.extend(a[i : i + na])
+        i += na
+        steps.extend(b[j : j + nb])
+        j += nb
+    return steps
 
 
 def tile_feedforward_pb_kernel(
@@ -70,162 +58,240 @@ def tile_feedforward_pb_kernel(
     with ExitStack() as ctx:
         const = ctx.enter_context(tc.tile_pool(name="const", bufs=1))
         keep = ctx.enter_context(tc.tile_pool(name="keep", bufs=1))
-        stage = ctx.enter_context(tc.tile_pool(name="stage", bufs=2))
+        stage = ctx.enter_context(tc.tile_pool(name="stage", bufs=3))
         small = ctx.enter_context(tc.tile_pool(name="small", bufs=1))
-        psum_t = ctx.enter_context(tc.psum_pool(name="psum_t", bufs=4))
-        psum_acc = ctx.enter_context(tc.psum_pool(name="psum_acc", bufs=4))
+        psum_t = ctx.enter_context(tc.psum_pool(name="psum_t", bufs=3))
+        psum_acc = ctx.enter_context(tc.psum_pool(name="psum_acc", bufs=5))
+        if PIN == "all":
+            ctx.enter_context(tc.manual_schedule())
+        if PIN == "pe":
+            ctx.enter_context(tc.manual_schedule(engines={mybir.EngineType.PE}))
 
         ident = const.tile([P, P], F32)
         make_identity(nc, ident[:])
+        ones_bf = const.tile([P, 2 * P], BF16)
+        nc.vector.memset(ones_bf[:], 1.0)
         eps = const.tile([P, 1], F32)
         nc.vector.memset(eps[:], EPS)
         warm = const.tile([P, 1], F32)
         nc.scalar.activation(out=warm[:], in_=eps[:], func=ACT.Sqrt)
 
-        fv_raw = keep.tile([P, NODE_TILES, DV * F_VEC], BF16)
-        fs_raw = keep.tile([P, NODE_TILES, F_SCAL], BF16)
-        hv_raw = keep.tile([P, NODE_TILES, DV * H_VEC], BF16)
-        hs_raw = keep.tile([P, NODE_TILES, H_SCAL], BF16)
-        b1 = keep.tile([P, FV_BLOCKS, PAIR, O_VEC], BF16)
-        b0 = keep.tile([P, FS_UNITS, PAIR, O_SCAL], BF16)
-        w1_raw = keep.tile([P, V_PASSES, PACK, O_VEC], BF16)
-        w0_raw = keep.tile([P, S_PASSES, PACK, O_SCAL], BF16)
-
-        def load_node_tiles(tile, columns):
-            for nt in range(NODE_TILES):
-                nc.sync.dma_start(out=tile[:, nt, :], in_=columns[nt * P : (nt + 1) * P, :])
-
-        def load_mx_weight(tile, weight, passes):
-            for g in range(passes):
-                nc.sync.dma_start(
-                    out=tile[:, g].rearrange("p (u e) c -> p u (e c)", e=PAIR),
-                    in_=weight[g * K_PASS : (g + 1) * K_PASS, :].rearrange("(u p e) c -> p u (e c)", p=P, e=PAIR),
-                )
-
-        def load_plain_weight(tile, weight):
-            nc.sync.dma_start(
-                out=tile[:].rearrange("p b e c -> p b (e c)"),
-                in_=weight.rearrange("(b p e) c -> p b (e c)", p=P, e=PAIR),
-            )
-
         W_ROWS = (O_SCAL + O_VEC) // P
         B_ROWS = O_SCAL // P
         bn_rows = const.tile([P, P], BF16)
         nc.vector.memset(bn_rows[:], 0.0)
-        nc.sync.dma_start(out=bn_rows[0:W_ROWS, :], in_=bn_weight.rearrange("(r c) -> r c", c=P))
-        nc.sync.dma_start(out=bn_rows[W_ROWS : W_ROWS + B_ROWS, :], in_=bn_bias.rearrange("(r c) -> r c", c=P))
 
-        load_node_tiles(fv_raw, features[:, F_SCAL:])
-        load_node_tiles(hv_raw, h2[:, H_SCAL:])
-        load_plain_weight(b1, byp_W1)
-        load_mx_weight(w1_raw, lin3_W1, V_PASSES)
-        load_node_tiles(hs_raw, h2[:, :H_SCAL])
-        load_node_tiles(fs_raw, features[:, :F_SCAL])
-        load_plain_weight(b0, byp_W0)
-        load_mx_weight(w0_raw, lin3_W0, S_PASSES)
+        def node_tiles(name, width):
+            return [keep.tile([P, width], BF16, name="%s%d" % (name, nt)) for nt in range(NODE_TILES)]
+
+        fv_raw = node_tiles("fv_raw", DV * F_VEC)
+        fs_raw = node_tiles("fs_raw", F_SCAL)
+        hv_raw = node_tiles("hv_raw", DV * H_VEC)
+        hs_raw = node_tiles("hs_raw", H_SCAL)
+        b1 = keep.tile([P, FV_BLOCKS, PAIR, O_VEC], BF16)
+        b0 = [keep.tile([P, PAIR, O_SCAL], BF16, name="b0_%d" % b) for b in range(FS_UNITS)]
+        w1_raw = [keep.tile([P, PACK, O_VEC], BF16, name="w1_raw%d" % g) for g in range(V_PASSES)]
+        w0_raw = [keep.tile([P, PACK, O_SCAL], BF16, name="w0_raw%d" % g) for g in range(S_PASSES)]
+
+        def load_nodes(tiles, columns):
+            for nt in range(NODE_TILES):
+                nc.sync.dma_start(out=tiles[nt][:], in_=columns[nt * P : (nt + 1) * P, :])
+
+        def load_mx(tile, rows):
+            nc.sync.dma_start(
+                out=tile[:].rearrange("p (u e) c -> p u (e c)", e=PAIR),
+                in_=rows.rearrange("(u p e) c -> p u (e c)", p=P, e=PAIR),
+            )
+
+        loads = {
+            "fv": lambda: load_nodes(fv_raw, features[:, F_SCAL:]),
+            "fs": lambda: load_nodes(fs_raw, features[:, :F_SCAL]),
+            "hv": lambda: load_nodes(hv_raw, h2[:, H_SCAL:]),
+            "hs": lambda: load_nodes(hs_raw, h2[:, :H_SCAL]),
+            "b1": lambda: nc.sync.dma_start(
+                out=b1[:].rearrange("p b e c -> p b (e c)"), in_=byp_W1.rearrange("(b p e) c -> p b (e c)", p=P, e=PAIR)
+            ),
+        }
+
+        def load_bn():
+            nc.sync.dma_start(out=bn_rows[0:W_ROWS, :], in_=bn_weight.rearrange("(r c) -> r c", c=P))
+            nc.sync.dma_start(out=bn_rows[W_ROWS : W_ROWS + B_ROWS, :], in_=bn_bias.rearrange("(r c) -> r c", c=P))
+
+        loads["bn"] = load_bn
+
+        def load_b0(b):
+            nc.sync.dma_start(
+                out=b0[b][:].rearrange("p e c -> p (e c)"),
+                in_=byp_W0[b * K_WORDS : (b + 1) * K_WORDS, :].rearrange("(p e) c -> p (e c)", e=PAIR),
+            )
+
+        for name in ("fv", "b1", "bn", "w10", "w11", "hs", "hv", "w00", "fs", "w01", "b00", "b01", "w02", "b02", "b03", "w03"):
+            if name in loads:
+                loads[name]()
+            elif name[:2] == "b0":
+                load_b0(int(name[2]))
+            elif name[:2] == "w1":
+                g = int(name[2])
+                load_mx(w1_raw[g], lin3_W1[g * K_PASS : (g + 1) * K_PASS, :])
+            else:
+                g = int(name[2])
+                load_mx(w0_raw[g], lin3_W0[g * K_PASS : (g + 1) * K_PASS, :])
 
         f_t = keep.tile([P, FS_UNITS + DV * FV_BLOCKS, NODES, PAIR], BF16)
-
-        def features_units(first_unit, words_of_unit):
-            bank = psum_t.tile([P, 2, NODES], F32, tag="t")
-            for slot in range(2):
-                transpose_words(nc, bank, slot, words_of_unit(first_unit + slot), ident)
-            nc.scalar.copy(
-                out=f_t[:, first_unit : first_unit + 2].rearrange("p s n e -> p (s n e)"),
-                in_=bank[:].rearrange("p s n -> p (s n)").bitcast(BF16),
-            )
-
-        def vector_words(unit):
-            b, r = divmod(unit - FS_UNITS, DV)
-            first = DV * P * b + r
-            return lambda nt: fv_raw[:, nt, :].bitcast(F32)[:, first : first + DV * (P - 1) + 1 : DV]
-
-        def scalar_words(unit):
-            return lambda nt: fs_raw[:, nt, :].bitcast(F32)[:, unit * P : (unit + 1) * P]
-
-        for first_unit in range(FS_UNITS, FS_UNITS + DV * FV_BLOCKS, 2):
-            features_units(first_unit, vector_words)
-
+        hv_sorted = [keep.tile([P, DV, H_VEC], BF16, name="hv_sorted%d" % nt) for nt in range(NODE_TILES)]
         h_codes = keep.tile([P, H_UNITS, NODES], U32, align_bytes=64)
         h_scales = keep.tile([P, H_UNITS, NODES], U8, align_bytes=64)
-
-        def transpose_h2_unit(words_of_half):
-            bank = psum_t.tile([P, 2, NODES], F32, tag="t")
-            for u in range(2):
-                transpose_words(nc, bank, u, words_of_half(u), ident)
-            grouped = stage.tile([P, NODES * PACK], BF16, align_bytes=64, tag="h_grouped", bufs=4)
-            nc.scalar.copy(
-                out=grouped[:].bitcast(F32).rearrange("p (n u) -> p n u", u=2),
-                in_=bank[:].rearrange("p u n -> p n u"),
-            )
-            return grouped
-
-        def quantise_h2_unit(unit, grouped):
-            quantise(nc, grouped[:], h_codes[:, unit, :], h_scales[:, unit, :])
-
-        hv_sorted = keep.tile([P, NODE_TILES, DV, H_VEC], BF16)
-        for nt in range(NODE_TILES):
-            nc.vector.tensor_copy(out=hv_sorted[:, nt], in_=hv_raw[:, nt, :].rearrange("p (i d) -> p d i", d=DV))
-
-        def h2_vector_words(g, d):
-            def words_of_half(u):
-                first = (PAIR * g + u) * P
-                return lambda nt: hv_sorted[:, nt, d, :].bitcast(F32)[:, first : first + P]
-
-            return words_of_half
-
-        def h2_scalar_words(g):
-            def words_of_half(u):
-                first = (PAIR * g + u) * P
-                return lambda nt: hs_raw[:, nt, :].bitcast(F32)[:, first : first + P]
-
-            return words_of_half
-
         w1_codes = keep.tile([P, V_PASSES, O_VEC], U32, align_bytes=64)
         w1_scales = keep.tile([P, V_PASSES, O_VEC], U8, align_bytes=64)
-        for g in range(V_PASSES):
-            w1_grouped = regroup_weight_pass(nc, stage, w1_raw[:, g])
-            quantise(nc, w1_grouped[:].rearrange("p c t -> p (c t)"), w1_codes[:, g, :], w1_scales[:, g, :])
-
-        for g in range(V_PASSES):
-            for d in range(DV):
-                quantise_h2_unit(S_PASSES + DV * g + d, transpose_h2_unit(h2_vector_words(g, d)))
-
+        w0_codes = keep.tile([P, S_PASSES, O_SCAL], U32, align_bytes=64)
+        w0_scales = keep.tile([P, S_PASSES, O_SCAL], U8, align_bytes=64)
         y_v = keep.tile([P, V_TILES, DV, NODES], F32)
-        for ct in range(V_TILES):
-            chans = slice(ct * P, (ct + 1) * P)
-            acc01 = psum_acc.tile([P, 2, NODES], F32, tag="acc")
-            acc2 = psum_acc.tile([P, 1, NODES], F32, tag="acc")
-            for d in range(DV):
-                acc = acc01[:, d, :] if d < 2 else acc2[:, 0, :]
-                for b in range(FV_BLOCKS):
-                    for e in range(PAIR):
-                        r, half = divmod(DV * e + d, PAIR)
-                        nc.tensor.matmul(
-                            out=acc,
-                            lhsT=b1[:, b, e, chans],
-                            rhs=f_t[:, FS_UNITS + DV * b + r, :, half],
-                            start=(b == 0 and e == 0),
-                            stop=(b == FV_BLOCKS - 1 and e == PAIR - 1),
-                        )
-            nc.scalar.activation(out=y_v[:, ct, 0:2, :], in_=acc01[:], func=ACT.Copy, scale=F_VEC**-0.5)
-            nc.scalar.activation(out=y_v[:, ct, 2:3, :], in_=acc2[:], func=ACT.Copy, scale=F_VEC**-0.5)
+        y_s = keep.tile([P, S_TILES, NODES], F32)
+        out_v = keep.tile([P, NODE_TILES, DV * O_VEC], F32)
+        out_s = keep.tile([P, NODE_TILES, O_SCAL], F32)
+        out_by_tile = out.rearrange("(nt p) c -> p nt c", p=P)
 
-        bn_rows_f32 = const.tile([P, P], F32)
-        nc.vector.tensor_copy(out=bn_rows_f32[:], in_=bn_rows[:])
-        bn_bank = psum_t.tile([P, P], F32, tag="t")
-        nc.tensor.transpose(bn_bank[:], bn_rows_f32[:], ident[:])
-        bn_cols = const.tile([P, W_ROWS + B_ROWS], F32)
-        nc.vector.tensor_copy(out=bn_cols[:], in_=bn_bank[:, : W_ROWS + B_ROWS])
-        weight_s = bn_cols[:, 0:S_TILES]
-        weight_v = bn_cols[:, S_TILES:W_ROWS]
-        bias_s = bn_cols[:, W_ROWS : W_ROWS + B_ROWS]
+        engines = {"v": nc.vector, "s": nc.scalar, "g": nc.gpsimd}
+
+        def copy_on(which, dst, src):
+            if which == "v":
+                nc.vector.tensor_copy(out=dst, in_=src)
+            elif which == "s":
+                nc.scalar.copy(out=dst, in_=src)
+            else:
+                nc.gpsimd.tensor_scalar(out=dst, in0=src, scalar1=1.0, scalar2=0.0, op0=ALU.mult, op1=ALU.add)
+
+        def quantise(grouped, codes, scales):
+            nc.vector.quantize_mx(out=codes.bitcast(FP8X4), scales=scales, in_=grouped)
+
+        def regroup(raw, s_cols):
+            width = raw.shape[2]
+            grouped = stage.tile([P, width, PACK], BF16, align_bytes=64, tag="w_grouped", bufs=3)
+            split = width - s_cols
+            if s_cols:
+                nc.scalar.copy(
+                    out=grouped[:, split:, :].rearrange("p (c i) t -> p c t i", i=4),
+                    in_=raw[:, :, split:].rearrange("p t (c i) -> p c t i", i=4),
+                )
+            if split:
+                nc.vector.tensor_copy(
+                    out=grouped[:, :split, :].rearrange("p (c i) t -> p c t i", i=4),
+                    in_=raw[:, :, :split].rearrange("p t (c i) -> p c t i", i=4),
+                )
+            return grouped[:].rearrange("p c t -> p (c t)")
+
+        def weight_w1(g, s_cols):
+            grouped = regroup(w1_raw[g][:], s_cols)
+            return lambda: quantise(grouped, w1_codes[:, g, :], w1_scales[:, g, :])
+
+        def weight_w0(g, h, s_cols):
+            cols = slice(h * HALF, (h + 1) * HALF)
+            grouped = regroup(w0_raw[g][:, :, cols], s_cols)
+            return lambda: quantise(grouped, w0_codes[:, g, cols], w0_scales[:, g, cols])
+
+        def t_steps(bank, words_of, finish):
+            def one(slot, nt):
+                return lambda: nc.tensor.transpose(bank[:, slot, nt * P : (nt + 1) * P], words_of(slot, nt), ident[:])
+
+            steps = [one(slot, nt) for slot in range(2) for nt in range(NODE_TILES)]
+            return steps[:-1] + [lambda: (steps[-1](), finish())]
+
+        def features_units(first_unit, words_of_unit, who):
+            def make():
+                bank = psum_t.tile([P, 2, NODES], F32, tag="t")
+                return t_steps(
+                    bank,
+                    lambda slot, nt: words_of_unit(first_unit + slot, nt),
+                    lambda: copy_on(
+                        who,
+                        f_t[:, first_unit : first_unit + 2].rearrange("p s n e -> p (s n e)").bitcast(F32),
+                        bank[:].rearrange("p s n -> p (s n)"),
+                    ),
+                )
+
+            return (4, make)
+
+        def fv_words(unit, nt):
+            b, r = divmod(unit - FS_UNITS, DV)
+            first = DV * P * b + r
+            return fv_raw[nt][:].bitcast(F32)[:, first : first + DV * (P - 1) + 1 : DV]
+
+        def fs_words(unit, nt):
+            return fs_raw[nt][:].bitcast(F32)[:, unit * P : (unit + 1) * P]
+
+        pending_q = []
+
+        def h2_unit(unit, words_of_half, who):
+            def make():
+                bank = psum_t.tile([P, 2, NODES], F32, tag="t")
+                grouped = stage.tile([P, NODES * PACK], BF16, align_bytes=64, tag="h_grouped", bufs=4)
+
+                def finish():
+                    copy_on(
+                        who,
+                        grouped[:].bitcast(F32).rearrange("p (n u) -> p n u", u=2),
+                        bank[:].rearrange("p u n -> p n u"),
+                    )
+                    pending_q.append(lambda: quantise(grouped[:], h_codes[:, unit, :], h_scales[:, unit, :]))
+
+                return t_steps(bank, words_of_half, finish)
+
+            return (4, make)
+
+        def hv_unit(g, d, who):
+            return h2_unit(
+                S_PASSES + DV * g + d,
+                lambda u, nt: hv_sorted[nt][:, d, :].bitcast(F32)[:, (PAIR * g + u) * P : (PAIR * g + u + 1) * P],
+                who,
+            )
+
+        def hs_unit(g, who):
+            return h2_unit(
+                g, lambda u, nt: hs_raw[nt][:].bitcast(F32)[:, (PAIR * g + u) * P : (PAIR * g + u + 1) * P], who
+            )
+
+        def flush_q():
+            for q in pending_q:
+                q()
+            pending_q.clear()
+
+        def sort_hv(nt, d):
+            copy_on(SORT_ENGINES[d], hv_sorted[nt][:, d, :], hv_raw[nt][:].rearrange("p (i d) -> p d i", d=DV)[:, d, :])
+
+        def bypass_v(ct):
+            def make():
+                chans = slice(ct * P, (ct + 1) * P)
+                acc01 = psum_acc.tile([P, 2, NODES], F32, tag="acc")
+                acc2 = psum_acc.tile([P, 1, NODES], F32, tag="acc")
+
+                def one(d, b, e):
+                    acc = acc01[:, d, :] if d < 2 else acc2[:, 0, :]
+                    r, half = divmod(DV * e + d, PAIR)
+                    return lambda: nc.tensor.matmul(
+                        out=acc,
+                        lhsT=b1[:, b, e, chans],
+                        rhs=f_t[:, FS_UNITS + DV * b + r, :, half],
+                        start=(b == 0 and e == 0),
+                        stop=(b == FV_BLOCKS - 1 and e == PAIR - 1),
+                    )
+
+                steps = [one(d, b, e) for d in range(DV) for b in range(FV_BLOCKS) for e in range(PAIR)]
+                steps[7] = (lambda f: lambda: (
+                    f(), nc.scalar.activation(out=y_v[:, ct, 0:2, :], in_=acc01[:], func=ACT.Copy, scale=F_VEC**-0.5)
+                ))(steps[7])
+                steps[11] = (lambda f: lambda: (
+                    f(), nc.scalar.activation(out=y_v[:, ct, 2:3, :], in_=acc2[:], func=ACT.Copy, scale=F_VEC**-0.5)
+                ))(steps[11])
+                return steps
+
+            return (12, make)
 
         sumsq_v = small.tile([P, V_TILES], F32)
         std_v = small.tile([P, V_TILES], F32)
         rstd_v = small.tile([P, V_TILES], F32)
         gain_v = small.tile([P, V_TILES], F32)
-        for ct in range(V_TILES):
+
+        def mx_v(ct):
             chans = slice(ct * P, (ct + 1) * P)
             acc01 = psum_acc.tile([P, 2, NODES], F32, tag="acc")
             acc2 = psum_acc.tile([P, 1, NODES], F32, tag="acc")
@@ -245,65 +311,94 @@ def tile_feedforward_pb_kernel(
                 nc.vector.scalar_tensor_tensor(
                     out=part, in0=acc[:], scalar=H_VEC**-0.5, in1=part, op0=ALU.mult, op1=ALU.add
                 )
-            squares = stage.tile([P, DV, NODES], BF16, tag="squares", bufs=4)
+            squares = stage.tile([P, DV, NODES], BF16, tag="squares", bufs=2)
+            nc.scalar.activation(out=squares[:], in_=y_v[:, ct], func=ACT.Square, accum_out=sumsq_v[:, ct : ct + 1])
+
+        def bn_columns():
+            bn_rows_f32 = const.tile([P, P], F32)
+            nc.vector.tensor_copy(out=bn_rows_f32[:], in_=bn_rows[:])
+            bn_bank = psum_t.tile([P, P], F32, tag="t")
+            nc.tensor.transpose(bn_bank[:], bn_rows_f32[:], ident[:])
+            bn_cols = const.tile([P, W_ROWS + B_ROWS], F32)
+            nc.vector.tensor_copy(out=bn_cols[:], in_=bn_bank[:, : W_ROWS + B_ROWS])
+            return bn_cols
+
+        def gains_v(first_ct, n):
+            grp = slice(first_ct, first_ct + n)
             nc.scalar.activation(
-                out=squares[:], in_=y_v[:, ct], func=ACT.Square, accum_out=sumsq_v[:, ct : ct + 1]
+                out=std_v[:, grp], in_=sumsq_v[:, grp], func=ACT.Sqrt, scale=1.0 / (DV * NODES), bias=eps[:]
+            )
+            nc.vector.reciprocal(out=rstd_v[:, grp], in_=std_v[:, grp])
+            nc.vector.tensor_mul(out=gain_v[:, grp], in0=rstd_v[:, grp], in1=weight_v[:, grp])
+
+        def norm_v(ct):
+            engines["v"].tensor_scalar(
+                out=y_v[:, ct], in0=y_v[:, ct], scalar1=gain_v[:, ct : ct + 1], scalar2=0.0, op0=ALU.mult, op1=ALU.add
             )
 
-        nc.scalar.activation(out=std_v[:], in_=sumsq_v[:], func=ACT.Sqrt, scale=1.0 / (DV * NODES), bias=eps[:])
-        nc.vector.reciprocal(out=rstd_v[:], in_=std_v[:])
-        nc.vector.tensor_mul(out=gain_v[:], in0=rstd_v[:], in1=weight_v)
-
-        for first_unit in range(0, FS_UNITS, 2):
-            features_units(first_unit, scalar_words)
-        for g in range(S_PASSES):
-            quantise_h2_unit(g, transpose_h2_unit(h2_scalar_words(g)))
-
-        w0_codes = keep.tile([P, S_PASSES, O_SCAL], U32, align_bytes=64)
-        w0_scales = keep.tile([P, S_PASSES, O_SCAL], U8, align_bytes=64)
-        for g in range(S_PASSES):
-            w0_grouped = regroup_weight_pass(nc, stage, w0_raw[:, g])
-            quantise(nc, w0_grouped[:].rearrange("p c t -> p (c t)"), w0_codes[:, g, :], w0_scales[:, g, :])
-
-        y_s = keep.tile([P, S_TILES, NODES], F32)
-        for pair_ct in range(0, S_TILES, 2):
-            acc = psum_acc.tile([P, 2, NODES], F32, tag="acc")
-            for j in range(2):
-                chans = slice((pair_ct + j) * P, (pair_ct + j + 1) * P)
-                for b in range(FS_UNITS):
-                    for e in range(PAIR):
-                        nc.tensor.matmul(
-                            out=acc[:, j, :],
-                            lhsT=b0[:, b, e, chans],
-                            rhs=f_t[:, b, :, e],
-                            start=(b == 0 and e == 0),
-                            stop=(b == FS_UNITS - 1 and e == PAIR - 1),
-                        )
-            nc.scalar.activation(out=y_s[:, pair_ct : pair_ct + 2, :], in_=acc[:], func=ACT.Copy, scale=F_SCAL**-0.5)
-
-        out_v = keep.tile([P, NODE_TILES, DV * O_VEC], F32)
-        for ct in range(V_TILES):
-            nc.scalar.activation(out=y_v[:, ct], in_=y_v[:, ct], func=ACT.Copy, scale=gain_v[:, ct : ct + 1])
-            for nt in range(NODE_TILES):
+        def back_v(ct, nt):
+            def make():
                 back = psum_t.tile([P, DV, P], F32, tag="t")
-                for d in range(DV):
-                    nc.tensor.transpose(back[:, d, :], y_v[:, ct, d, nt * P : (nt + 1) * P], ident[:])
-                nc.scalar.copy(
-                    out=out_v[:, nt, DV * P * ct : DV * P * (ct + 1)].rearrange("p (o d) -> p o d", d=DV),
-                    in_=back[:].rearrange("p d o -> p o d"),
+
+                def one(d):
+                    return lambda: nc.tensor.transpose(back[:, d, :], y_v[:, ct, d, nt * P : (nt + 1) * P], ident[:])
+
+                def finish():
+                    one(DV - 1)()
+                    cols = slice(DV * P * ct, DV * P * (ct + 1))
+                    nc.scalar.copy(
+                        out=out_v[:, nt, cols].rearrange("p (o d) -> p o d", d=DV), in_=back[:].rearrange("p d o -> p o d")
+                    )
+                    if nt == NODE_TILES - 1:
+                        nc.sync.dma_start(
+                            out=out_by_tile[:, :, O_SCAL + DV * P * ct : O_SCAL + DV * P * (ct + 1)], in_=out_v[:, :, cols]
+                        )
+
+                return [one(0), one(1), finish]
+
+            return (3, make)
+
+        def bypass_s(pair_ct):
+            def make():
+                acc = psum_acc.tile([P, 2, NODES], F32, tag="acc")
+
+                def one(j, b, e):
+                    c = (pair_ct + j) * P
+                    return lambda: nc.tensor.matmul(
+                        out=acc[:, j, :],
+                        lhsT=b0[b][:, e, c : c + P],
+                        rhs=f_t[:, b, :, e],
+                        start=(b == 0 and e == 0),
+                        stop=(b == FS_UNITS - 1 and e == PAIR - 1),
+                    )
+
+                steps = [one(j, b, e) for j in range(2) for b in range(FS_UNITS) for e in range(PAIR)]
+                last = steps[-1]
+                steps[-1] = lambda: (
+                    last(),
+                    nc.scalar.activation(
+                        out=y_s[:, pair_ct : pair_ct + 2, :], in_=acc[:], func=ACT.Copy, scale=F_SCAL**-0.5
+                    ),
                 )
-        for nt in range(NODE_TILES):
-            nc.sync.dma_start(out=out[nt * P : (nt + 1) * P, O_SCAL:], in_=out_v[:, nt, :])
+                return steps
+
+            return (16, make)
 
         BN_STATS = 6
         stats_s = small.tile([P, S_TILES, BN_STATS], F32)
         mean_var_s = small.tile([P, S_TILES, 2], F32)
-        for pair_ct in range(0, S_TILES, 2):
-            acc = psum_acc.tile([P, 2, NODES], F32, tag="acc")
-            for j in range(2):
-                chans = slice((pair_ct + j) * P, (pair_ct + j + 1) * P)
-                for g in range(S_PASSES):
-                    nc.tensor.matmul_mx(
+        std_s = small.tile([P, S_TILES], F32)
+        rstd_s = small.tile([P, S_TILES], F32)
+        gain_s = small.tile([P, S_TILES], F32)
+        shift_s = small.tile([P, S_TILES], F32)
+
+        def mx_s(pair_ct):
+            def make():
+                acc = psum_acc.tile([P, 2, NODES], F32, tag="acc")
+
+                def one(j, g):
+                    chans = slice((pair_ct + j) * P, (pair_ct + j + 1) * P)
+                    return lambda: nc.tensor.matmul_mx(
                         out=acc[:, j, :],
                         lhsT=w0_codes[:, g, chans].bitcast(FP8X4),
                         lhsT_scale=w0_scales[:, g, chans],
@@ -312,41 +407,117 @@ def tile_feedforward_pb_kernel(
                         start=(g == 0),
                         stop=(g == S_PASSES - 1),
                     )
-            pair = slice(pair_ct, pair_ct + 2)
-            nc.vector.scalar_tensor_tensor(
-                out=y_s[:, pair, :], in0=acc[:], scalar=H_SCAL**-0.5, in1=y_s[:, pair, :], op0=ALU.mult, op1=ALU.add
-            )
-            for ct in (pair_ct, pair_ct + 1):
-                nc.vector.bn_stats(out=stats_s[:, ct, :], in_=y_s[:, ct, :])
-                nc.vector.bn_aggr(out=mean_var_s[:, ct, :], in_=stats_s[:, ct, :])
 
-        out_s = keep.tile([P, NODE_TILES, O_SCAL], F32)
-        std_s = small.tile([P, S_TILES], F32)
-        rstd_s = small.tile([P, S_TILES], F32)
-        gain_s = small.tile([P, S_TILES], F32)
-        shift_s = small.tile([P, S_TILES], F32)
-        out_by_tile = out.rearrange("(nt p) c -> p nt c", p=P)
-        for first_ct in range(0, S_TILES, QUAD):
-            quad = slice(first_ct, first_ct + QUAD)
-            nc.scalar.activation(out=std_s[:, quad], in_=mean_var_s[:, quad, 1], func=ACT.Sqrt, bias=eps[:])
-            nc.vector.reciprocal(out=rstd_s[:, quad], in_=std_s[:, quad])
-            nc.vector.tensor_mul(out=gain_s[:, quad], in0=rstd_s[:, quad], in1=weight_s[:, quad])
-            nc.vector.tensor_mul(out=shift_s[:, quad], in0=mean_var_s[:, quad, 0], in1=gain_s[:, quad])
-            nc.vector.tensor_sub(out=shift_s[:, quad], in0=bias_s[:, quad], in1=shift_s[:, quad])
-            for pair_ct in range(first_ct, first_ct + QUAD, 2):
-                back = psum_t.tile([P, NODE_TILES, 2, P], F32, tag="t")
-                for j in range(2):
-                    ct = pair_ct + j
-                    nc.vector.tensor_scalar(
-                        out=y_s[:, ct, :],
-                        in0=y_s[:, ct, :],
-                        scalar1=gain_s[:, ct : ct + 1],
-                        scalar2=shift_s[:, ct : ct + 1],
+                def finish():
+                    one(1, S_PASSES - 1)()
+                    pair = slice(pair_ct, pair_ct + 2)
+                    nc.vector.scalar_tensor_tensor(
+                        out=y_s[:, pair, :],
+                        in0=acc[:],
+                        scalar=H_SCAL**-0.5,
+                        in1=y_s[:, pair, :],
                         op0=ALU.mult,
                         op1=ALU.add,
                     )
-                    for nt in range(NODE_TILES):
-                        nc.tensor.transpose(back[:, nt, j, :], y_s[:, ct, nt * P : (nt + 1) * P], ident[:])
-                cols = slice(pair_ct * P, (pair_ct + 2) * P)
-                nc.scalar.copy(out=out_s[:, :, cols], in_=back[:].rearrange("p nt j c -> p nt (j c)"))
-                nc.sync.dma_start(out=out_by_tile[:, :, cols], in_=out_s[:, :, cols])
+                    for ct in (pair_ct, pair_ct + 1):
+                        nc.vector.bn_stats(out=stats_s[:, ct, :], in_=y_s[:, ct, :])
+                        nc.vector.bn_aggr(out=mean_var_s[:, ct, :], in_=stats_s[:, ct, :])
+                    gains_s(pair_ct, 2)
+                    norm_s(pair_ct)
+
+                steps = [one(j, g) for j in range(2) for g in range(S_PASSES)]
+                return steps[:-1] + [finish]
+
+            return (8, make)
+
+        def gains_s(first_ct, n):
+            grp = slice(first_ct, first_ct + n)
+            nc.scalar.activation(out=std_s[:, grp], in_=mean_var_s[:, grp, 1], func=ACT.Sqrt, bias=eps[:])
+            nc.vector.reciprocal(out=rstd_s[:, grp], in_=std_s[:, grp])
+            nc.vector.tensor_mul(out=gain_s[:, grp], in0=rstd_s[:, grp], in1=weight_s[:, grp])
+            nc.vector.tensor_mul(out=shift_s[:, grp], in0=mean_var_s[:, grp, 0], in1=gain_s[:, grp])
+            nc.vector.tensor_sub(out=shift_s[:, grp], in0=bias_s[:, grp], in1=shift_s[:, grp])
+
+        def norm_s(pair_ct):
+            for ct in (pair_ct, pair_ct + 1):
+                engines["v"].tensor_scalar(
+                    out=y_s[:, ct, :],
+                    in0=y_s[:, ct, :],
+                    scalar1=gain_s[:, ct : ct + 1],
+                    scalar2=shift_s[:, ct : ct + 1],
+                    op0=ALU.mult,
+                    op1=ALU.add,
+                )
+
+        def back_s(pair_ct):
+            def make():
+                back = psum_t.tile([P, NODE_TILES, 2, P], F32, tag="t")
+
+                def one(j, nt):
+                    return lambda: nc.tensor.transpose(
+                        back[:, nt, j, :], y_s[:, pair_ct + j, nt * P : (nt + 1) * P], ident[:]
+                    )
+
+                def finish():
+                    one(1, 1)()
+                    cols = slice(pair_ct * P, (pair_ct + 2) * P)
+                    nc.scalar.copy(out=out_s[:, :, cols], in_=back[:].rearrange("p nt j c -> p nt (j c)"))
+                    nc.sync.dma_start(out=out_by_tile[:, :, cols], in_=out_s[:, :, cols])
+
+                return [one(0, 0), one(0, 1), one(1, 0), finish]
+
+            return (4, make)
+
+        def warm_up(n):
+            junk = psum_acc.tile([P, 2 * P], F32, tag="acc")
+            for i in range(n):
+                nc.tensor.matmul(out=junk[:], lhsT=ones_bf[:, :P], rhs=ones_bf[:], start=True, stop=True)
+
+        def lazy(jobs):
+            steps = []
+            for n, make in jobs:
+                box = []
+                steps.extend([(lambda i=i, make=make, box=box: (box or box.extend(make()), box[i]())) for i in range(n)])
+            return steps
+
+        def run(steps):
+            for step in steps:
+                step()
+
+        run(lazy([features_units(u, fv_words, "s") for u in (4, 6, 8)]))
+        for nt in range(NODE_TILES):
+            for d in range(DV):
+                sort_hv(nt, d)
+        BV = [lazy([bypass_v(ct)]) for ct in range(V_TILES)]
+        BS = [lazy([bypass_s(p)]) for p in range(0, S_TILES, 2)]
+        TS = lazy([hs_unit(g, "sv"[g % 2]) for g in range(S_PASSES)])
+        run(weave(BV[0] + BV[1], TS, 6, 4))
+        bn_cols = bn_columns()
+        weight_s = bn_cols[:, 0:S_TILES]
+        weight_v = bn_cols[:, S_TILES:W_ROWS]
+        bias_s = bn_cols[:, W_ROWS : W_ROWS + B_ROWS]
+        flush_q()
+        qs = [weight_w1(g, S_COLS) for g in range(V_PASSES)]
+        for q in qs:
+            q()
+        TH = lazy([hv_unit(g, d, "sv"[(DV * g + d) % 2]) for g in range(V_PASSES) for d in range(DV)])
+        run(weave(BV[2] + BV[3], TH, 4, 4))
+        flush_q()
+        run(lazy([features_units(u, fs_words, "s") for u in (0, 2)]))
+        run(BS[0])
+        for ct in range(V_TILES):
+            mx_v(ct)
+            if ct % 2:
+                gains_v(ct - 1, 2)
+                norm_v(ct - 1)
+                norm_v(ct)
+        for g in range(S_PASSES):
+            qs = [weight_w0(g, h, S_COLS) for h in range(2)]
+            for q in qs:
+                q()
+        RV = lazy([back_v(ct, nt) for ct in range(V_TILES) for nt in range(NODE_TILES)])
+        run(BS[1])
+        run(weave(BS[2] + BS[3], RV, 4, 3))
+        XS = [lazy([mx_s(p)]) for p in range(0, S_TILES, 2)]
+        RS = [lazy([back_s(p)]) for p in range(0, S_TILES, 2)]
+        run(XS[0] + XS[1] + XS[2] + RS[0] + XS[3] + RS[1] + RS[2] + RS[3])

@@ -60,8 +60,8 @@ def tile_feedforward_pb_kernel(
         keep = ctx.enter_context(tc.tile_pool(name="keep", bufs=1))
         stage = ctx.enter_context(tc.tile_pool(name="stage", bufs=3))
         small = ctx.enter_context(tc.tile_pool(name="small", bufs=1))
-        psum_t = ctx.enter_context(tc.psum_pool(name="psum_t", bufs=3))
-        psum_acc = ctx.enter_context(tc.psum_pool(name="psum_acc", bufs=5))
+        psum_t = ctx.enter_context(tc.psum_pool(name="psum_t", bufs=4))
+        psum_acc = ctx.enter_context(tc.psum_pool(name="psum_acc", bufs=4))
         if PIN == "all":
             ctx.enter_context(tc.manual_schedule())
         if PIN == "pe":
@@ -125,7 +125,7 @@ def tile_feedforward_pb_kernel(
                 in_=byp_W0[b * K_WORDS : (b + 1) * K_WORDS, :].rearrange("(p e) c -> p (e c)", e=PAIR),
             )
 
-        for name in ("fv", "b1", "bn", "w10", "w11", "hs", "hv", "w00", "fs", "w01", "b00", "b01", "w02", "b02", "b03", "w03"):
+        for name in ("fv", "b1", "bn", "w10", "w11", "hs", "hv", "w00", "fs", "b00", "b01", "b02", "b03", "w01", "w02", "w03"):
             if name in loads:
                 loads[name]()
             elif name[:2] == "b0":
@@ -212,7 +212,7 @@ def tile_feedforward_pb_kernel(
             return (4, make)
 
         def fv_words(unit, nt):
-            b, r = divmod(unit - FS_UNITS, DV)
+            r, b = divmod(unit - FS_UNITS, FV_BLOCKS)
             first = DV * P * b + r
             return fv_raw[nt][:].bitcast(F32)[:, first : first + DV * (P - 1) + 1 : DV]
 
@@ -270,7 +270,7 @@ def tile_feedforward_pb_kernel(
                     return lambda: nc.tensor.matmul(
                         out=acc,
                         lhsT=b1[:, b, e, chans],
-                        rhs=f_t[:, FS_UNITS + DV * b + r, :, half],
+                        rhs=f_t[:, FS_UNITS + FV_BLOCKS * r + b, :, half],
                         start=(b == 0 and e == 0),
                         stop=(b == FV_BLOCKS - 1 and e == PAIR - 1),
                     )

@@ -74,7 +74,7 @@ def tile_feedforward_pb_kernel(
         eps = const.tile([P, 1], F32)
         nc.vector.memset(eps[:], EPS)
         warm = const.tile([P, 1], F32)
-        nc.scalar.activation(out=warm[:], in_=eps[:], func=ACT.Sqrt)
+        nc.scalar.activation(out=warm[:], in_=eps[:], func=ACT.Abs_reciprocal_sqrt)
 
         W_ROWS = (O_SCAL + O_VEC) // P
         B_ROWS = O_SCAL // P
@@ -287,7 +287,6 @@ def tile_feedforward_pb_kernel(
             return (12, make)
 
         sumsq_v = small.tile([P, V_TILES], F32)
-        std_v = small.tile([P, V_TILES], F32)
         rstd_v = small.tile([P, V_TILES], F32)
         gain_v = small.tile([P, V_TILES], F32)
 
@@ -326,9 +325,12 @@ def tile_feedforward_pb_kernel(
         def gains_v(first_ct, n):
             grp = slice(first_ct, first_ct + n)
             nc.scalar.activation(
-                out=std_v[:, grp], in_=sumsq_v[:, grp], func=ACT.Sqrt, scale=1.0 / (DV * NODES), bias=eps[:]
+                out=rstd_v[:, grp],
+                in_=sumsq_v[:, grp],
+                func=ACT.Abs_reciprocal_sqrt,
+                scale=1.0 / (DV * NODES),
+                bias=eps[:],
             )
-            nc.vector.reciprocal(out=rstd_v[:, grp], in_=std_v[:, grp])
             nc.vector.tensor_mul(out=gain_v[:, grp], in0=rstd_v[:, grp], in1=weight_v[:, grp])
 
         def norm_v(ct):
@@ -387,7 +389,7 @@ def tile_feedforward_pb_kernel(
         BN_STATS = 6
         stats_s = small.tile([P, S_TILES, BN_STATS], F32)
         mean_var_s = small.tile([P, S_TILES, 2], F32)
-        std_s = small.tile([P, S_TILES], F32)
+        mean_w_s = small.tile([P, S_TILES], F32)
         rstd_s = small.tile([P, S_TILES], F32)
         gain_s = small.tile([P, S_TILES], F32)
         shift_s = small.tile([P, S_TILES], F32)
@@ -410,17 +412,19 @@ def tile_feedforward_pb_kernel(
 
                 def finish():
                     one(1, S_PASSES - 1)()
-                    pair = slice(pair_ct, pair_ct + 2)
-                    nc.vector.scalar_tensor_tensor(
-                        out=y_s[:, pair, :],
-                        in0=acc[:],
-                        scalar=H_SCAL**-0.5,
-                        in1=y_s[:, pair, :],
-                        op0=ALU.mult,
-                        op1=ALU.add,
-                    )
-                    for ct in (pair_ct, pair_ct + 1):
+                    cts = (pair_ct, pair_ct + 1)
+                    for j, ct in enumerate(cts):
+                        nc.vector.scalar_tensor_tensor(
+                            out=y_s[:, ct, :],
+                            in0=acc[:, j, :],
+                            scalar=H_SCAL**-0.5,
+                            in1=y_s[:, ct, :],
+                            op0=ALU.mult,
+                            op1=ALU.add,
+                        )
+                    for ct in cts:
                         nc.vector.bn_stats(out=stats_s[:, ct, :], in_=y_s[:, ct, :])
+                    for ct in cts:
                         nc.vector.bn_aggr(out=mean_var_s[:, ct, :], in_=stats_s[:, ct, :])
                     gains_s(pair_ct, 2)
                     norm_s(pair_ct)
@@ -432,10 +436,12 @@ def tile_feedforward_pb_kernel(
 
         def gains_s(first_ct, n):
             grp = slice(first_ct, first_ct + n)
-            nc.scalar.activation(out=std_s[:, grp], in_=mean_var_s[:, grp, 1], func=ACT.Sqrt, bias=eps[:])
-            nc.vector.reciprocal(out=rstd_s[:, grp], in_=std_s[:, grp])
+            nc.scalar.activation(
+                out=rstd_s[:, grp], in_=mean_var_s[:, grp, 1], func=ACT.Abs_reciprocal_sqrt, bias=eps[:]
+            )
+            nc.vector.tensor_mul(out=mean_w_s[:, grp], in0=mean_var_s[:, grp, 0], in1=weight_s[:, grp])
+            nc.vector.tensor_mul(out=shift_s[:, grp], in0=mean_w_s[:, grp], in1=rstd_s[:, grp])
             nc.vector.tensor_mul(out=gain_s[:, grp], in0=rstd_s[:, grp], in1=weight_s[:, grp])
-            nc.vector.tensor_mul(out=shift_s[:, grp], in0=mean_var_s[:, grp, 0], in1=gain_s[:, grp])
             nc.vector.tensor_sub(out=shift_s[:, grp], in0=bias_s[:, grp], in1=shift_s[:, grp])
 
         def norm_s(pair_ct):

@@ -522,8 +522,8 @@ def tile_feedforward_pb_kernel(
             for q in qs:
                 q()
         RV = lazy([back_v(ct, nt) for ct in range(V_TILES) for nt in range(NODE_TILES)])
-        run(BS[1])
-        run(weave(BS[2] + BS[3], RV, 4, 3))
+        run(BS[1] + BS[2])
+        run(weave(BS[3], RV[:12], 4, 3))
         XS = [lazy([mx_s(p)]) for p in range(0, S_TILES, 2)]
         RS = [lazy([back_s(p)]) for p in range(0, S_TILES, 2)]
-        run(XS[0] + XS[1] + XS[2] + RS[0] + XS[3] + RS[1] + RS[2] + RS[3])
+        run(XS[0] + XS[1] + XS[2] + XS[3] + RV[12:18] + RS[0] + RV[18:] + RS[1] + RS[2] + RS[3])

@@ -38,7 +38,7 @@ FLOPS = 2 * NODES * (H_SCAL + F_SCAL) * O_SCAL + 2 * NODES * DV * (H_VEC + F_VEC
 
 PIN = "none"
 SORT_ENGINES = ("v", "s", "g")
-S_COLS = 160
+S_COLS = 224
 
 
 def weave(a, b, na, nb):

@@ -32,13 +32,14 @@ V_TILES = O_VEC // P
 FS_UNITS = F_SCAL // K_WORDS
 FV_BLOCKS = F_VEC // K_WORDS
 H_UNITS = S_PASSES + DV * V_PASSES
-HALF = 512
+W_ROWS = (O_SCAL + O_VEC) // P
+B_ROWS = O_SCAL // P
+BN_STATS = 6
+
+CHUNK = 512
+SCALAR_COLS = 224
 
 FLOPS = 2 * NODES * (H_SCAL + F_SCAL) * O_SCAL + 2 * NODES * DV * (H_VEC + F_VEC) * O_VEC
-
-PIN = "none"
-SORT_ENGINES = ("v", "s", "g")
-S_COLS = 224
 
 
 def weave(a, b, na, nb):
@@ -49,6 +50,19 @@ def weave(a, b, na, nb):
         steps.extend(b[j : j + nb])
         j += nb
     return steps
+
+
+def steps_of(jobs):
+    steps = []
+    for n, make in jobs:
+        made = []
+        steps.extend([(lambda i=i, make=make, made=made: (made or made.extend(make()), made[i]())) for i in range(n)])
+    return steps
+
+
+def run(steps):
+    for step in steps:
+        step()
 
 
 def tile_feedforward_pb_kernel(
@@ -62,22 +76,13 @@ def tile_feedforward_pb_kernel(
         small = ctx.enter_context(tc.tile_pool(name="small", bufs=1))
         psum_t = ctx.enter_context(tc.psum_pool(name="psum_t", bufs=4))
         psum_acc = ctx.enter_context(tc.psum_pool(name="psum_acc", bufs=4))
-        if PIN == "all":
-            ctx.enter_context(tc.manual_schedule())
-        if PIN == "pe":
-            ctx.enter_context(tc.manual_schedule(engines={mybir.EngineType.PE}))
 
         ident = const.tile([P, P], F32)
         make_identity(nc, ident[:])
-        ones_bf = const.tile([P, 2 * P], BF16)
-        nc.vector.memset(ones_bf[:], 1.0)
         eps = const.tile([P, 1], F32)
         nc.vector.memset(eps[:], EPS)
         warm = const.tile([P, 1], F32)
         nc.scalar.activation(out=warm[:], in_=eps[:], func=ACT.Abs_reciprocal_sqrt)
-
-        W_ROWS = (O_SCAL + O_VEC) // P
-        B_ROWS = O_SCAL // P
         bn_rows = const.tile([P, P], BF16)
         nc.vector.memset(bn_rows[:], 0.0)
 
@@ -97,45 +102,31 @@ def tile_feedforward_pb_kernel(
             for nt in range(NODE_TILES):
                 nc.sync.dma_start(out=tiles[nt][:], in_=columns[nt * P : (nt + 1) * P, :])
 
-        def load_mx(tile, rows):
+        def load_mx_pass(tile, weight, g):
             nc.sync.dma_start(
                 out=tile[:].rearrange("p (u e) c -> p u (e c)", e=PAIR),
-                in_=rows.rearrange("(u p e) c -> p u (e c)", p=P, e=PAIR),
+                in_=weight[g * K_PASS : (g + 1) * K_PASS, :].rearrange("(u p e) c -> p u (e c)", p=P, e=PAIR),
             )
 
-        loads = {
-            "fv": lambda: load_nodes(fv_raw, features[:, F_SCAL:]),
-            "fs": lambda: load_nodes(fs_raw, features[:, :F_SCAL]),
-            "hv": lambda: load_nodes(hv_raw, h2[:, H_SCAL:]),
-            "hs": lambda: load_nodes(hs_raw, h2[:, :H_SCAL]),
-            "b1": lambda: nc.sync.dma_start(
-                out=b1[:].rearrange("p b e c -> p b (e c)"), in_=byp_W1.rearrange("(b p e) c -> p b (e c)", p=P, e=PAIR)
-            ),
-        }
-
-        def load_bn():
-            nc.sync.dma_start(out=bn_rows[0:W_ROWS, :], in_=bn_weight.rearrange("(r c) -> r c", c=P))
-            nc.sync.dma_start(out=bn_rows[W_ROWS : W_ROWS + B_ROWS, :], in_=bn_bias.rearrange("(r c) -> r c", c=P))
-
-        loads["bn"] = load_bn
-
-        def load_b0(b):
+        load_nodes(fv_raw, features[:, F_SCAL:])
+        nc.sync.dma_start(
+            out=b1[:].rearrange("p b e c -> p b (e c)"), in_=byp_W1.rearrange("(b p e) c -> p b (e c)", p=P, e=PAIR)
+        )
+        nc.sync.dma_start(out=bn_rows[0:W_ROWS, :], in_=bn_weight.rearrange("(r c) -> r c", c=P))
+        nc.sync.dma_start(out=bn_rows[W_ROWS : W_ROWS + B_ROWS, :], in_=bn_bias.rearrange("(r c) -> r c", c=P))
+        for g in range(V_PASSES):
+            load_mx_pass(w1_raw[g], lin3_W1, g)
+        load_nodes(hs_raw, h2[:, :H_SCAL])
+        load_nodes(hv_raw, h2[:, H_SCAL:])
+        load_mx_pass(w0_raw[0], lin3_W0, 0)
+        load_nodes(fs_raw, features[:, :F_SCAL])
+        for b in range(FS_UNITS):
             nc.sync.dma_start(
                 out=b0[b][:].rearrange("p e c -> p (e c)"),
                 in_=byp_W0[b * K_WORDS : (b + 1) * K_WORDS, :].rearrange("(p e) c -> p (e c)", e=PAIR),
             )
-
-        for name in ("fv", "b1", "bn", "w10", "w11", "hs", "hv", "w00", "fs", "b00", "b01", "b02", "b03", "w01", "w02", "w03"):
-            if name in loads:
-                loads[name]()
-            elif name[:2] == "b0":
-                load_b0(int(name[2]))
-            elif name[:2] == "w1":
-                g = int(name[2])
-                load_mx(w1_raw[g], lin3_W1[g * K_PASS : (g + 1) * K_PASS, :])
-            else:
-                g = int(name[2])
-                load_mx(w0_raw[g], lin3_W0[g * K_PASS : (g + 1) * K_PASS, :])
+        for g in range(1, S_PASSES):
+            load_mx_pass(w0_raw[g], lin3_W0, g)
 
         f_t = keep.tile([P, FS_UNITS + DV * FV_BLOCKS, NODES, PAIR], BF16)
         hv_sorted = [keep.tile([P, DV, H_VEC], BF16, name="hv_sorted%d" % nt) for nt in range(NODE_TILES)]
@@ -151,12 +142,10 @@ def tile_feedforward_pb_kernel(
         out_s = keep.tile([P, NODE_TILES, O_SCAL], F32)
         out_by_tile = out.rearrange("(nt p) c -> p nt c", p=P)
 
-        engines = {"v": nc.vector, "s": nc.scalar, "g": nc.gpsimd}
-
-        def copy_on(which, dst, src):
-            if which == "v":
+        def copy_on(engine, dst, src):
+            if engine == "v":
                 nc.vector.tensor_copy(out=dst, in_=src)
-            elif which == "s":
+            elif engine == "s":
                 nc.scalar.copy(out=dst, in_=src)
             else:
                 nc.gpsimd.tensor_scalar(out=dst, in0=src, scalar1=1.0, scalar2=0.0, op0=ALU.mult, op1=ALU.add)
@@ -164,46 +153,40 @@ def tile_feedforward_pb_kernel(
         def quantise(grouped, codes, scales):
             nc.vector.quantize_mx(out=codes.bitcast(FP8X4), scales=scales, in_=grouped)
 
-        def regroup(raw, s_cols):
-            width = raw.shape[2]
-            grouped = stage.tile([P, width, PACK], BF16, align_bytes=64, tag="w_grouped", bufs=3)
-            split = width - s_cols
-            if s_cols:
-                nc.scalar.copy(
-                    out=grouped[:, split:, :].rearrange("p (c i) t -> p c t i", i=4),
-                    in_=raw[:, :, split:].rearrange("p t (c i) -> p c t i", i=4),
-                )
-            if split:
-                nc.vector.tensor_copy(
-                    out=grouped[:, :split, :].rearrange("p (c i) t -> p c t i", i=4),
-                    in_=raw[:, :, :split].rearrange("p t (c i) -> p c t i", i=4),
+        def regroup(raw):
+            grouped = stage.tile([P, CHUNK, PACK], BF16, align_bytes=64, tag="w_grouped", bufs=3)
+            for engine, cols in (("s", slice(CHUNK - SCALAR_COLS, CHUNK)), ("v", slice(0, CHUNK - SCALAR_COLS))):
+                copy_on(
+                    engine,
+                    grouped[:, cols, :].rearrange("p (c i) t -> p c t i", i=4),
+                    raw[:, :, cols].rearrange("p t (c i) -> p c t i", i=4),
                 )
             return grouped[:].rearrange("p c t -> p (c t)")
 
-        def weight_w1(g, s_cols):
-            grouped = regroup(w1_raw[g][:], s_cols)
-            return lambda: quantise(grouped, w1_codes[:, g, :], w1_scales[:, g, :])
+        def quantise_weight(chunks):
+            regrouped = [regroup(raw) for raw, codes, scales in chunks]
+            for (raw, codes, scales), grouped in zip(chunks, regrouped):
+                quantise(grouped, codes, scales)
 
-        def weight_w0(g, h, s_cols):
-            cols = slice(h * HALF, (h + 1) * HALF)
-            grouped = regroup(w0_raw[g][:, :, cols], s_cols)
-            return lambda: quantise(grouped, w0_codes[:, g, cols], w0_scales[:, g, cols])
+        def w0_pass(g):
+            both = [slice(first, first + CHUNK) for first in range(0, O_SCAL, CHUNK)]
+            quantise_weight([(w0_raw[g][:, :, cols], w0_codes[:, g, cols], w0_scales[:, g, cols]) for cols in both])
 
-        def t_steps(bank, words_of, finish):
+        def four_transposes(bank, words_of, empty):
             def one(slot, nt):
                 return lambda: nc.tensor.transpose(bank[:, slot, nt * P : (nt + 1) * P], words_of(slot, nt), ident[:])
 
             steps = [one(slot, nt) for slot in range(2) for nt in range(NODE_TILES)]
-            return steps[:-1] + [lambda: (steps[-1](), finish())]
+            return steps[:-1] + [lambda: (steps[-1](), empty())]
 
-        def features_units(first_unit, words_of_unit, who):
+        def features_units(first_unit, words_of_unit):
             def make():
                 bank = psum_t.tile([P, 2, NODES], F32, tag="t")
-                return t_steps(
+                return four_transposes(
                     bank,
                     lambda slot, nt: words_of_unit(first_unit + slot, nt),
                     lambda: copy_on(
-                        who,
+                        "s",
                         f_t[:, first_unit : first_unit + 2].rearrange("p s n e -> p (s n e)").bitcast(F32),
                         bank[:].rearrange("p s n -> p (s n)"),
                     ),
@@ -219,44 +202,38 @@ def tile_feedforward_pb_kernel(
         def fs_words(unit, nt):
             return fs_raw[nt][:].bitcast(F32)[:, unit * P : (unit + 1) * P]
 
-        pending_q = []
+        to_quantise = []
 
-        def h2_unit(unit, words_of_half, who):
+        def h2_unit(unit, words_of_part):
             def make():
                 bank = psum_t.tile([P, 2, NODES], F32, tag="t")
                 grouped = stage.tile([P, NODES * PACK], BF16, align_bytes=64, tag="h_grouped", bufs=4)
 
-                def finish():
+                def empty():
                     copy_on(
-                        who,
+                        "sv"[unit % 2],
                         grouped[:].bitcast(F32).rearrange("p (n u) -> p n u", u=2),
                         bank[:].rearrange("p u n -> p n u"),
                     )
-                    pending_q.append(lambda: quantise(grouped[:], h_codes[:, unit, :], h_scales[:, unit, :]))
+                    to_quantise.append(lambda: quantise(grouped[:], h_codes[:, unit, :], h_scales[:, unit, :]))
 
-                return t_steps(bank, words_of_half, finish)
+                return four_transposes(bank, words_of_part, empty)
 
             return (4, make)
 
-        def hv_unit(g, d, who):
-            return h2_unit(
-                S_PASSES + DV * g + d,
-                lambda u, nt: hv_sorted[nt][:, d, :].bitcast(F32)[:, (PAIR * g + u) * P : (PAIR * g + u + 1) * P],
-                who,
-            )
+        def pass_words(rows, g, u):
+            return rows.bitcast(F32)[:, (PAIR * g + u) * P : (PAIR * g + u + 1) * P]
 
-        def hs_unit(g, who):
-            return h2_unit(
-                g, lambda u, nt: hs_raw[nt][:].bitcast(F32)[:, (PAIR * g + u) * P : (PAIR * g + u + 1) * P], who
-            )
+        def hs_unit(g):
+            return h2_unit(g, lambda u, nt: pass_words(hs_raw[nt][:], g, u))
 
-        def flush_q():
-            for q in pending_q:
-                q()
-            pending_q.clear()
+        def hv_unit(g, d):
+            return h2_unit(S_PASSES + DV * g + d, lambda u, nt: pass_words(hv_sorted[nt][:, d, :], g, u))
 
-        def sort_hv(nt, d):
-            copy_on(SORT_ENGINES[d], hv_sorted[nt][:, d, :], hv_raw[nt][:].rearrange("p (i d) -> p d i", d=DV)[:, d, :])
+        def quantise_waiting():
+            for call in to_quantise:
+                call()
+            to_quantise.clear()
 
         def bypass_v(ct):
             def make():
@@ -265,26 +242,30 @@ def tile_feedforward_pb_kernel(
                 acc2 = psum_acc.tile([P, 1, NODES], F32, tag="acc")
 
                 def one(d, b, e):
-                    acc = acc01[:, d, :] if d < 2 else acc2[:, 0, :]
                     r, half = divmod(DV * e + d, PAIR)
                     return lambda: nc.tensor.matmul(
-                        out=acc,
+                        out=acc01[:, d, :] if d < 2 else acc2[:, 0, :],
                         lhsT=b1[:, b, e, chans],
                         rhs=f_t[:, FS_UNITS + FV_BLOCKS * r + b, :, half],
                         start=(b == 0 and e == 0),
                         stop=(b == FV_BLOCKS - 1 and e == PAIR - 1),
                     )
 
+                def then_empty(step, acc, first_d, n_d):
+                    return lambda: (
+                        step(),
+                        nc.scalar.activation(
+                            out=y_v[:, ct, first_d : first_d + n_d, :], in_=acc[:], func=ACT.Copy, scale=F_VEC**-0.5
+                        ),
+                    )
+
                 steps = [one(d, b, e) for d in range(DV) for b in range(FV_BLOCKS) for e in range(PAIR)]
-                steps[7] = (lambda f: lambda: (
-                    f(), nc.scalar.activation(out=y_v[:, ct, 0:2, :], in_=acc01[:], func=ACT.Copy, scale=F_VEC**-0.5)
-                ))(steps[7])
-                steps[11] = (lambda f: lambda: (
-                    f(), nc.scalar.activation(out=y_v[:, ct, 2:3, :], in_=acc2[:], func=ACT.Copy, scale=F_VEC**-0.5)
-                ))(steps[11])
+                per_d = FV_BLOCKS * PAIR
+                steps[2 * per_d - 1] = then_empty(steps[2 * per_d - 1], acc01, 0, 2)
+                steps[3 * per_d - 1] = then_empty(steps[3 * per_d - 1], acc2, 2, 1)
                 return steps
 
-            return (12, make)
+            return (DV * FV_BLOCKS * PAIR, make)
 
         sumsq_v = small.tile([P, V_TILES], F32)
         rstd_v = small.tile([P, V_TILES], F32)
@@ -313,80 +294,69 @@ def tile_feedforward_pb_kernel(
             squares = stage.tile([P, DV, NODES], BF16, tag="squares", bufs=2)
             nc.scalar.activation(out=squares[:], in_=y_v[:, ct], func=ACT.Square, accum_out=sumsq_v[:, ct : ct + 1])
 
-        def bn_columns():
-            bn_rows_f32 = const.tile([P, P], F32)
-            nc.vector.tensor_copy(out=bn_rows_f32[:], in_=bn_rows[:])
-            bn_bank = psum_t.tile([P, P], F32, tag="t")
-            nc.tensor.transpose(bn_bank[:], bn_rows_f32[:], ident[:])
-            bn_cols = const.tile([P, W_ROWS + B_ROWS], F32)
-            nc.vector.tensor_copy(out=bn_cols[:], in_=bn_bank[:, : W_ROWS + B_ROWS])
-            return bn_cols
-
-        def gains_v(first_ct, n):
-            grp = slice(first_ct, first_ct + n)
+        def norm_v(first_ct):
+            two = slice(first_ct, first_ct + 2)
             nc.scalar.activation(
-                out=rstd_v[:, grp],
-                in_=sumsq_v[:, grp],
+                out=rstd_v[:, two],
+                in_=sumsq_v[:, two],
                 func=ACT.Abs_reciprocal_sqrt,
                 scale=1.0 / (DV * NODES),
                 bias=eps[:],
             )
-            nc.vector.tensor_mul(out=gain_v[:, grp], in0=rstd_v[:, grp], in1=weight_v[:, grp])
-
-        def norm_v(ct):
-            engines["v"].tensor_scalar(
-                out=y_v[:, ct], in0=y_v[:, ct], scalar1=gain_v[:, ct : ct + 1], scalar2=0.0, op0=ALU.mult, op1=ALU.add
-            )
+            nc.vector.tensor_mul(out=gain_v[:, two], in0=rstd_v[:, two], in1=weight_v[:, two])
+            for ct in (first_ct, first_ct + 1):
+                nc.vector.tensor_scalar(
+                    out=y_v[:, ct], in0=y_v[:, ct], scalar1=gain_v[:, ct : ct + 1], scalar2=None, op0=ALU.mult
+                )
 
         def back_v(ct, nt):
             def make():
                 back = psum_t.tile([P, DV, P], F32, tag="t")
+                cols = slice(DV * P * ct, DV * P * (ct + 1))
 
                 def one(d):
                     return lambda: nc.tensor.transpose(back[:, d, :], y_v[:, ct, d, nt * P : (nt + 1) * P], ident[:])
 
-                def finish():
+                def last():
                     one(DV - 1)()
-                    cols = slice(DV * P * ct, DV * P * (ct + 1))
                     nc.scalar.copy(
                         out=out_v[:, nt, cols].rearrange("p (o d) -> p o d", d=DV), in_=back[:].rearrange("p d o -> p o d")
                     )
                     if nt == NODE_TILES - 1:
                         nc.sync.dma_start(
-                            out=out_by_tile[:, :, O_SCAL + DV * P * ct : O_SCAL + DV * P * (ct + 1)], in_=out_v[:, :, cols]
+                            out=out_by_tile[:, :, O_SCAL + cols.start : O_SCAL + cols.stop], in_=out_v[:, :, cols]
                         )
 
-                return [one(0), one(1), finish]
+                return [one(d) for d in range(DV - 1)] + [last]
 
-            return (3, make)
+            return (DV, make)
 
         def bypass_s(pair_ct):
             def make():
                 acc = psum_acc.tile([P, 2, NODES], F32, tag="acc")
 
                 def one(j, b, e):
-                    c = (pair_ct + j) * P
+                    first = (pair_ct + j) * P
                     return lambda: nc.tensor.matmul(
                         out=acc[:, j, :],
-                        lhsT=b0[b][:, e, c : c + P],
+                        lhsT=b0[b][:, e, first : first + P],
                         rhs=f_t[:, b, :, e],
                         start=(b == 0 and e == 0),
                         stop=(b == FS_UNITS - 1 and e == PAIR - 1),
                     )
 
                 steps = [one(j, b, e) for j in range(2) for b in range(FS_UNITS) for e in range(PAIR)]
-                last = steps[-1]
-                steps[-1] = lambda: (
-                    last(),
-                    nc.scalar.activation(
-                        out=y_s[:, pair_ct : pair_ct + 2, :], in_=acc[:], func=ACT.Copy, scale=F_SCAL**-0.5
-                    ),
-                )
-                return steps
+                return steps[:-1] + [
+                    lambda: (
+                        steps[-1](),
+                        nc.scalar.activation(
+                            out=y_s[:, pair_ct : pair_ct + 2, :], in_=acc[:], func=ACT.Copy, scale=F_SCAL**-0.5
+                        ),
+                    )
+                ]
 
-            return (16, make)
+            return (2 * FS_UNITS * PAIR, make)
 
-        BN_STATS = 6
         stats_s = small.tile([P, S_TILES, BN_STATS], F32)
         mean_var_s = small.tile([P, S_TILES, 2], F32)
         mean_w_s = small.tile([P, S_TILES], F32)
@@ -397,6 +367,8 @@ def tile_feedforward_pb_kernel(
         def mx_s(pair_ct):
             def make():
                 acc = psum_acc.tile([P, 2, NODES], F32, tag="acc")
+                tiles = (pair_ct, pair_ct + 1)
+                two = slice(pair_ct, pair_ct + 2)
 
                 def one(j, g):
                     chans = slice((pair_ct + j) * P, (pair_ct + j + 1) * P)
@@ -410,10 +382,9 @@ def tile_feedforward_pb_kernel(
                         stop=(g == S_PASSES - 1),
                     )
 
-                def finish():
+                def last():
                     one(1, S_PASSES - 1)()
-                    cts = (pair_ct, pair_ct + 1)
-                    for j, ct in enumerate(cts):
+                    for j, ct in enumerate(tiles):
                         nc.vector.scalar_tensor_tensor(
                             out=y_s[:, ct, :],
                             in0=acc[:, j, :],
@@ -422,108 +393,103 @@ def tile_feedforward_pb_kernel(
                             op0=ALU.mult,
                             op1=ALU.add,
                         )
-                    for ct in cts:
+                    for ct in tiles:
                         nc.vector.bn_stats(out=stats_s[:, ct, :], in_=y_s[:, ct, :])
-                    for ct in cts:
+                    for ct in tiles:
                         nc.vector.bn_aggr(out=mean_var_s[:, ct, :], in_=stats_s[:, ct, :])
-                    gains_s(pair_ct, 2)
-                    norm_s(pair_ct)
+                    nc.scalar.activation(
+                        out=rstd_s[:, two], in_=mean_var_s[:, two, 1], func=ACT.Abs_reciprocal_sqrt, bias=eps[:]
+                    )
+                    nc.vector.tensor_mul(out=mean_w_s[:, two], in0=mean_var_s[:, two, 0], in1=weight_s[:, two])
+                    nc.vector.tensor_mul(out=shift_s[:, two], in0=mean_w_s[:, two], in1=rstd_s[:, two])
+                    nc.vector.tensor_mul(out=gain_s[:, two], in0=rstd_s[:, two], in1=weight_s[:, two])
+                    nc.vector.tensor_sub(out=shift_s[:, two], in0=bias_s[:, two], in1=shift_s[:, two])
+                    for ct in tiles:
+                        nc.vector.tensor_scalar(
+                            out=y_s[:, ct, :],
+                            in0=y_s[:, ct, :],
+                            scalar1=gain_s[:, ct : ct + 1],
+                            scalar2=shift_s[:, ct : ct + 1],
+                            op0=ALU.mult,
+                            op1=ALU.add,
+                        )
 
-                steps = [one(j, g) for j in range(2) for g in range(S_PASSES)]
-                return steps[:-1] + [finish]
+                return [one(j, g) for j in range(2) for g in range(S_PASSES)][:-1] + [last]
 
-            return (8, make)
-
-        def gains_s(first_ct, n):
-            grp = slice(first_ct, first_ct + n)
-            nc.scalar.activation(
-                out=rstd_s[:, grp], in_=mean_var_s[:, grp, 1], func=ACT.Abs_reciprocal_sqrt, bias=eps[:]
-            )
-            nc.vector.tensor_mul(out=mean_w_s[:, grp], in0=mean_var_s[:, grp, 0], in1=weight_s[:, grp])
-            nc.vector.tensor_mul(out=shift_s[:, grp], in0=mean_w_s[:, grp], in1=rstd_s[:, grp])
-            nc.vector.tensor_mul(out=gain_s[:, grp], in0=rstd_s[:, grp], in1=weight_s[:, grp])
-            nc.vector.tensor_sub(out=shift_s[:, grp], in0=bias_s[:, grp], in1=shift_s[:, grp])
-
-        def norm_s(pair_ct):
-            for ct in (pair_ct, pair_ct + 1):
-                engines["v"].tensor_scalar(
-                    out=y_s[:, ct, :],
-                    in0=y_s[:, ct, :],
-                    scalar1=gain_s[:, ct : ct + 1],
-                    scalar2=shift_s[:, ct : ct + 1],
-                    op0=ALU.mult,
-                    op1=ALU.add,
-                )
+            return (2 * S_PASSES, make)
 
         def back_s(pair_ct):
             def make():
                 back = psum_t.tile([P, NODE_TILES, 2, P], F32, tag="t")
+                cols = slice(pair_ct * P, (pair_ct + 2) * P)
 
                 def one(j, nt):
                     return lambda: nc.tensor.transpose(
                         back[:, nt, j, :], y_s[:, pair_ct + j, nt * P : (nt + 1) * P], ident[:]
                     )
 
-                def finish():
-                    one(1, 1)()
-                    cols = slice(pair_ct * P, (pair_ct + 2) * P)
+                steps = [one(j, nt) for j in range(2) for nt in range(NODE_TILES)]
+
+                def last():
+                    steps[-1]()
                     nc.scalar.copy(out=out_s[:, :, cols], in_=back[:].rearrange("p nt j c -> p nt (j c)"))
                     nc.sync.dma_start(out=out_by_tile[:, :, cols], in_=out_s[:, :, cols])
 
-                return [one(0, 0), one(0, 1), one(1, 0), finish]
+                return steps[:-1] + [last]
 
-            return (4, make)
+            return (2 * NODE_TILES, make)
 
-        def warm_up(n):
-            junk = psum_acc.tile([P, 2 * P], F32, tag="acc")
-            for i in range(n):
-                nc.tensor.matmul(out=junk[:], lhsT=ones_bf[:, :P], rhs=ones_bf[:], start=True, stop=True)
+        pairs = range(0, S_TILES, 2)
+        bypass_v_steps = [steps_of([bypass_v(ct)]) for ct in range(V_TILES)]
+        bypass_s_steps = [steps_of([bypass_s(pair_ct)]) for pair_ct in pairs]
 
-        def lazy(jobs):
-            steps = []
-            for n, make in jobs:
-                box = []
-                steps.extend([(lambda i=i, make=make, box=box: (box or box.extend(make()), box[i]())) for i in range(n)])
-            return steps
+        run(steps_of([features_units(FS_UNITS + FV_BLOCKS * r, fv_words) for r in range(DV)]))
 
-        def run(steps):
-            for step in steps:
-                step()
-
-        run(lazy([features_units(u, fv_words, "s") for u in (4, 6, 8)]))
         for nt in range(NODE_TILES):
             for d in range(DV):
-                sort_hv(nt, d)
-        BV = [lazy([bypass_v(ct)]) for ct in range(V_TILES)]
-        BS = [lazy([bypass_s(p)]) for p in range(0, S_TILES, 2)]
-        TS = lazy([hs_unit(g, "sv"[g % 2]) for g in range(S_PASSES)])
-        run(weave(BV[0] + BV[1], TS, 6, 4))
-        bn_cols = bn_columns()
+                copy_on("vsg"[d], hv_sorted[nt][:, d, :], hv_raw[nt][:].rearrange("p (i d) -> p d i", d=DV)[:, d, :])
+
+        run(weave(bypass_v_steps[0] + bypass_v_steps[1], steps_of([hs_unit(g) for g in range(S_PASSES)]), 6, 4))
+
+        bn_rows_f32 = const.tile([P, P], F32)
+        nc.vector.tensor_copy(out=bn_rows_f32[:], in_=bn_rows[:])
+        bn_bank = psum_t.tile([P, P], F32, tag="t")
+        nc.tensor.transpose(bn_bank[:], bn_rows_f32[:], ident[:])
+        bn_cols = const.tile([P, W_ROWS + B_ROWS], F32)
+        nc.vector.tensor_copy(out=bn_cols[:], in_=bn_bank[:, : W_ROWS + B_ROWS])
         weight_s = bn_cols[:, 0:S_TILES]
         weight_v = bn_cols[:, S_TILES:W_ROWS]
         bias_s = bn_cols[:, W_ROWS : W_ROWS + B_ROWS]
-        flush_q()
-        qs = [weight_w1(g, S_COLS) for g in range(V_PASSES)]
-        for q in qs:
-            q()
-        TH = lazy([hv_unit(g, d, "sv"[(DV * g + d) % 2]) for g in range(V_PASSES) for d in range(DV)])
-        run(weave(BV[2] + BV[3], TH, 4, 4))
-        flush_q()
-        run(lazy([features_units(u, fs_words, "s") for u in (0, 2)]))
-        run(BS[0])
+
+        quantise_waiting()
+        quantise_weight([(w1_raw[g][:], w1_codes[:, g, :], w1_scales[:, g, :]) for g in range(V_PASSES)])
+        run(
+            weave(
+                bypass_v_steps[2] + bypass_v_steps[3],
+                steps_of([hv_unit(g, d) for g in range(V_PASSES) for d in range(DV)]),
+                4,
+                4,
+            )
+        )
+        quantise_waiting()
+
+        run(steps_of([features_units(unit, fs_words) for unit in range(0, FS_UNITS, 2)]))
+        run(bypass_s_steps[0])
+
         for ct in range(V_TILES):
             mx_v(ct)
             if ct % 2:
-                gains_v(ct - 1, 2)
                 norm_v(ct - 1)
-                norm_v(ct)
+
         for g in range(S_PASSES):
-            qs = [weight_w0(g, h, S_COLS) for h in range(2)]
-            for q in qs:
-                q()
-        RV = lazy([back_v(ct, nt) for ct in range(V_TILES) for nt in range(NODE_TILES)])
-        run(BS[1] + BS[2])
-        run(weave(BS[3], RV[:12], 4, 3))
-        XS = [lazy([mx_s(p)]) for p in range(0, S_TILES, 2)]
-        RS = [lazy([back_s(p)]) for p in range(0, S_TILES, 2)]
-        run(XS[0] + XS[1] + XS[2] + XS[3] + RV[12:18] + RS[0] + RV[18:] + RS[1] + RS[2] + RS[3])
+            w0_pass(g)
+
+        back_v_steps = [steps_of([back_v(ct, nt) for nt in range(NODE_TILES)]) for ct in range(V_TILES)]
+        run(bypass_s_steps[1] + bypass_s_steps[2])
+        run(weave(bypass_s_steps[3], back_v_steps[0] + back_v_steps[1], 4, 3))
+
+        for pair_ct in pairs:
+            run(steps_of([mx_s(pair_ct)]))
+        back_s_steps = [steps_of([back_s(pair_ct)]) for pair_ct in pairs]
+        run(back_v_steps[2] + back_s_steps[0] + back_v_steps[3])
+        run(back_s_steps[1] + back_s_steps[2] + back_s_steps[3])

from contextlib import ExitStack

import concourse.mybir as mybir
from concourse.masks import make_identity

F32 = mybir.dt.float32
BF16 = mybir.dt.bfloat16
U32 = mybir.dt.uint32
U8 = mybir.dt.uint8
FP8X4 = mybir.dt.float8_e4m3fn_x4
ACT = mybir.ActivationFunctionType
ALU = mybir.AluOpType

P = 128
NODES = 256
NODE_TILES = NODES // P
DV = 3
H_SCAL, H_VEC = 2048, 1024
F_SCAL, F_VEC = 1024, 512
O_SCAL, O_VEC = 1024, 512
EPS = 1e-5

PACK = 4
K_PASS = P * PACK
PAIR = 2
K_WORDS = P * PAIR

S_PASSES = H_SCAL // K_PASS
V_PASSES = H_VEC // K_PASS
S_TILES = O_SCAL // P
V_TILES = O_VEC // P
FS_UNITS = F_SCAL // K_WORDS
FV_BLOCKS = F_VEC // K_WORDS
H_UNITS = S_PASSES + DV * V_PASSES
W_ROWS = (O_SCAL + O_VEC) // P
B_ROWS = O_SCAL // P
BN_STATS = 6

CHUNK = 512
SCALAR_COLS = 224

FLOPS = 2 * NODES * (H_SCAL + F_SCAL) * O_SCAL + 2 * NODES * DV * (H_VEC + F_VEC) * O_VEC


def weave(a, b, na, nb):
    steps, i, j = [], 0, 0
    while i < len(a) or j < len(b):
        steps.extend(a[i : i + na])
        i += na
        steps.extend(b[j : j + nb])
        j += nb
    return steps


def steps_of(jobs):
    steps = []
    for n, make in jobs:
        made = []
        steps.extend([(lambda i=i, make=make, made=made: (made or made.extend(make()), made[i]())) for i in range(n)])
    return steps


def run(steps):
    for step in steps:
        step()


def tile_feedforward_pb_kernel(
    tc, h2, features, lin3_W0, lin3_W1, byp_W0, byp_W1, bn_weight, bn_bias, out
):
    nc = tc.nc
    with ExitStack() as ctx:
        const = ctx.enter_context(tc.tile_pool(name="const", bufs=1))
        keep = ctx.enter_context(tc.tile_pool(name="keep", bufs=1))
        stage = ctx.enter_context(tc.tile_pool(name="stage", bufs=3))
        small = ctx.enter_context(tc.tile_pool(name="small", bufs=1))
        psum_t = ctx.enter_context(tc.psum_pool(name="psum_t", bufs=4))
        psum_acc = ctx.enter_context(tc.psum_pool(name="psum_acc", bufs=4))

        ident = const.tile([P, P], F32)
        make_identity(nc, ident[:])
        eps = const.tile([P, 1], F32)
        nc.vector.memset(eps[:], EPS)
        warm = const.tile([P, 1], F32)
        nc.scalar.activation(out=warm[:], in_=eps[:], func=ACT.Abs_reciprocal_sqrt)
        bn_rows = const.tile([P, P], BF16)
        nc.vector.memset(bn_rows[:], 0.0)

        def node_tiles(name, width):
            return [keep.tile([P, width], BF16, name="%s%d" % (name, nt)) for nt in range(NODE_TILES)]

        fv_raw = node_tiles("fv_raw", DV * F_VEC)
        fs_raw = node_tiles("fs_raw", F_SCAL)
        hv_raw = node_tiles("hv_raw", DV * H_VEC)
        hs_raw = node_tiles("hs_raw", H_SCAL)
        b1 = keep.tile([P, FV_BLOCKS, PAIR, O_VEC], BF16)
        b0 = [keep.tile([P, PAIR, O_SCAL], BF16, name="b0_%d" % b) for b in range(FS_UNITS)]
        w1_raw = [keep.tile([P, PACK, O_VEC], BF16, name="w1_raw%d" % g) for g in range(V_PASSES)]
        w0_raw = [keep.tile([P, PACK, O_SCAL], BF16, name="w0_raw%d" % g) for g in range(S_PASSES)]

        def load_nodes(tiles, columns):
            for nt in range(NODE_TILES):
                nc.sync.dma_start(out=tiles[nt][:], in_=columns[nt * P : (nt + 1) * P, :])

        def load_mx_pass(tile, weight, g):
            nc.sync.dma_start(
                out=tile[:].rearrange("p (u e) c -> p u (e c)", e=PAIR),
                in_=weight[g * K_PASS : (g + 1) * K_PASS, :].rearrange("(u p e) c -> p u (e c)", p=P, e=PAIR),
            )

        load_nodes(fv_raw, features[:, F_SCAL:])
        nc.sync.dma_start(
            out=b1[:].rearrange("p b e c -> p b (e c)"), in_=byp_W1.rearrange("(b p e) c -> p b (e c)", p=P, e=PAIR)
        )
        nc.sync.dma_start(out=bn_rows[0:W_ROWS, :], in_=bn_weight.rearrange("(r c) -> r c", c=P))
        nc.sync.dma_start(out=bn_rows[W_ROWS : W_ROWS + B_ROWS, :], in_=bn_bias.rearrange("(r c) -> r c", c=P))
        for g in range(V_PASSES):
            load_mx_pass(w1_raw[g], lin3_W1, g)
        load_nodes(hs_raw, h2[:, :H_SCAL])
        load_nodes(hv_raw, h2[:, H_SCAL:])
        load_mx_pass(w0_raw[0], lin3_W0, 0)
        load_nodes(fs_raw, features[:, :F_SCAL])
        for b in range(FS_UNITS):
            nc.sync.dma_start(
                out=b0[b][:].rearrange("p e c -> p (e c)"),
                in_=byp_W0[b * K_WORDS : (b + 1) * K_WORDS, :].rearrange("(p e) c -> p (e c)", e=PAIR),
            )
        for g in range(1, S_PASSES):
            load_mx_pass(w0_raw[g], lin3_W0, g)

        f_t = keep.tile([P, FS_UNITS + DV * FV_BLOCKS, NODES, PAIR], BF16)
        hv_sorted = [keep.tile([P, DV, H_VEC], BF16, name="hv_sorted%d" % nt) for nt in range(NODE_TILES)]
        h_codes = keep.tile([P, H_UNITS, NODES], U32, align_bytes=64)
        h_scales = keep.tile([P, H_UNITS, NODES], U8, align_bytes=64)
        w1_codes = keep.tile([P, V_PASSES, O_VEC], U32, align_bytes=64)
        w1_scales = keep.tile([P, V_PASSES, O_VEC], U8, align_bytes=64)
        w0_codes = keep.tile([P, S_PASSES, O_SCAL], U32, align_bytes=64)
        w0_scales = keep.tile([P, S_PASSES, O_SCAL], U8, align_bytes=64)
        y_v = keep.tile([P, V_TILES, DV, NODES], F32)
        y_s = keep.tile([P, S_TILES, NODES], F32)
        out_v = keep.tile([P, NODE_TILES, DV * O_VEC], F32)
        out_s = keep.tile([P, NODE_TILES, O_SCAL], F32)
        out_by_tile = out.rearrange("(nt p) c -> p nt c", p=P)

        def copy_on(engine, dst, src):
            if engine == "v":
                nc.vector.tensor_copy(out=dst, in_=src)
            elif engine == "s":
                nc.scalar.copy(out=dst, in_=src)
            else:
                nc.gpsimd.tensor_scalar(out=dst, in0=src, scalar1=1.0, scalar2=0.0, op0=ALU.mult, op1=ALU.add)

        def quantise(grouped, codes, scales):
            nc.vector.quantize_mx(out=codes.bitcast(FP8X4), scales=scales, in_=grouped)

        def regroup(raw):
            grouped = stage.tile([P, CHUNK, PACK], BF16, align_bytes=64, tag="w_grouped", bufs=3)
            for engine, cols in (("s", slice(CHUNK - SCALAR_COLS, CHUNK)), ("v", slice(0, CHUNK - SCALAR_COLS))):
                copy_on(
                    engine,
                    grouped[:, cols, :].rearrange("p (c i) t -> p c t i", i=4),
                    raw[:, :, cols].rearrange("p t (c i) -> p c t i", i=4),
                )
            return grouped[:].rearrange("p c t -> p (c t)")

        def quantise_weight(chunks):
            regrouped = [regroup(raw) for raw, codes, scales in chunks]
            for (raw, codes, scales), grouped in zip(chunks, regrouped):
                quantise(grouped, codes, scales)

        def w0_pass(g):
            both = [slice(first, first + CHUNK) for first in range(0, O_SCAL, CHUNK)]
            quantise_weight([(w0_raw[g][:, :, cols], w0_codes[:, g, cols], w0_scales[:, g, cols]) for cols in both])

        def four_transposes(bank, words_of, empty):
            def one(slot, nt):
                return lambda: nc.tensor.transpose(bank[:, slot, nt * P : (nt + 1) * P], words_of(slot, nt), ident[:])

            steps = [one(slot, nt) for slot in range(2) for nt in range(NODE_TILES)]
            return steps[:-1] + [lambda: (steps[-1](), empty())]

        def features_units(first_unit, words_of_unit):
            def make():
                bank = psum_t.tile([P, 2, NODES], F32, tag="t")
                return four_transposes(
                    bank,
                    lambda slot, nt: words_of_unit(first_unit + slot, nt),
                    lambda: copy_on(
                        "s",
                        f_t[:, first_unit : first_unit + 2].rearrange("p s n e -> p (s n e)").bitcast(F32),
                        bank[:].rearrange("p s n -> p (s n)"),
                    ),
                )

            return (4, make)

        def fv_words(unit, nt):
            r, b = divmod(unit - FS_UNITS, FV_BLOCKS)
            first = DV * P * b + r
            return fv_raw[nt][:].bitcast(F32)[:, first : first + DV * (P - 1) + 1 : DV]

        def fs_words(unit, nt):
            return fs_raw[nt][:].bitcast(F32)[:, unit * P : (unit + 1) * P]

        to_quantise = []

        def h2_unit(unit, words_of_part):
            def make():
                bank = psum_t.tile([P, 2, NODES], F32, tag="t")
                grouped = stage.tile([P, NODES * PACK], BF16, align_bytes=64, tag="h_grouped", bufs=4)

                def empty():
                    copy_on(
                        "sv"[unit % 2],
                        grouped[:].bitcast(F32).rearrange("p (n u) -> p n u", u=2),
                        bank[:].rearrange("p u n -> p n u"),
                    )
                    to_quantise.append(lambda: quantise(grouped[:], h_codes[:, unit, :], h_scales[:, unit, :]))

                return four_transposes(bank, words_of_part, empty)

            return (4, make)

        def pass_words(rows, g, u):
            return rows.bitcast(F32)[:, (PAIR * g + u) * P : (PAIR * g + u + 1) * P]

        def hs_unit(g):
            return h2_unit(g, lambda u, nt: pass_words(hs_raw[nt][:], g, u))

        def hv_unit(g, d):
            return h2_unit(S_PASSES + DV * g + d, lambda u, nt: pass_words(hv_sorted[nt][:, d, :], g, u))

        def quantise_waiting():
            for call in to_quantise:
                call()
            to_quantise.clear()

        def bypass_v(ct):
            def make():
                chans = slice(ct * P, (ct + 1) * P)
                acc01 = psum_acc.tile([P, 2, NODES], F32, tag="acc")
                acc2 = psum_acc.tile([P, 1, NODES], F32, tag="acc")

                def one(d, b, e):
                    r, half = divmod(DV * e + d, PAIR)
                    return lambda: nc.tensor.matmul(
                        out=acc01[:, d, :] if d < 2 else acc2[:, 0, :],
                        lhsT=b1[:, b, e, chans],
                        rhs=f_t[:, FS_UNITS + FV_BLOCKS * r + b, :, half],
                        start=(b == 0 and e == 0),
                        stop=(b == FV_BLOCKS - 1 and e == PAIR - 1),
                    )

                def then_empty(step, acc, first_d, n_d):
                    return lambda: (
                        step(),
                        nc.scalar.activation(
                            out=y_v[:, ct, first_d : first_d + n_d, :], in_=acc[:], func=ACT.Copy, scale=F_VEC**-0.5
                        ),
                    )

                steps = [one(d, b, e) for d in range(DV) for b in range(FV_BLOCKS) for e in range(PAIR)]
                per_d = FV_BLOCKS * PAIR
                steps[2 * per_d - 1] = then_empty(steps[2 * per_d - 1], acc01, 0, 2)
                steps[3 * per_d - 1] = then_empty(steps[3 * per_d - 1], acc2, 2, 1)
                return steps

            return (DV * FV_BLOCKS * PAIR, make)

        sumsq_v = small.tile([P, V_TILES], F32)
        rstd_v = small.tile([P, V_TILES], F32)
        gain_v = small.tile([P, V_TILES], F32)

        def mx_v(ct):
            chans = slice(ct * P, (ct + 1) * P)
            acc01 = psum_acc.tile([P, 2, NODES], F32, tag="acc")
            acc2 = psum_acc.tile([P, 1, NODES], F32, tag="acc")
            for acc, first_d, n_d in ((acc01, 0, 2), (acc2, 2, 1)):
                for g in range(V_PASSES):
                    units = slice(S_PASSES + DV * g + first_d, S_PASSES + DV * g + first_d + n_d)
                    nc.tensor.matmul_mx(
                        out=acc[:].rearrange("p d n -> p (d n)"),
                        lhsT=w1_codes[:, g, chans].bitcast(FP8X4),
                        lhsT_scale=w1_scales[:, g, chans],
                        rhs=h_codes[:, units, :].rearrange("p d n -> p (d n)").bitcast(FP8X4),
                        rhs_scale=h_scales[:, units, :].rearrange("p d n -> p (d n)"),
                        start=(g == 0),
                        stop=(g == V_PASSES - 1),
                    )
                part = y_v[:, ct, first_d : first_d + n_d, :]
                nc.vector.scalar_tensor_tensor(
                    out=part, in0=acc[:], scalar=H_VEC**-0.5, in1=part, op0=ALU.mult, op1=ALU.add
                )
            squares = stage.tile([P, DV, NODES], BF16, tag="squares", bufs=2)
            nc.scalar.activation(out=squares[:], in_=y_v[:, ct], func=ACT.Square, accum_out=sumsq_v[:, ct : ct + 1])

        def norm_v(first_ct):
            two = slice(first_ct, first_ct + 2)
            nc.scalar.activation(
                out=rstd_v[:, two],
                in_=sumsq_v[:, two],
                func=ACT.Abs_reciprocal_sqrt,
                scale=1.0 / (DV * NODES),
                bias=eps[:],
            )
            nc.vector.tensor_mul(out=gain_v[:, two], in0=rstd_v[:, two], in1=weight_v[:, two])
            for ct in (first_ct, first_ct + 1):
                nc.vector.tensor_scalar(
                    out=y_v[:, ct], in0=y_v[:, ct], scalar1=gain_v[:, ct : ct + 1], scalar2=None, op0=ALU.mult
                )

        def back_v(ct, nt):
            def make():
                back = psum_t.tile([P, DV, P], F32, tag="t")
                cols = slice(DV * P * ct, DV * P * (ct + 1))

                def one(d):
                    return lambda: nc.tensor.transpose(back[:, d, :], y_v[:, ct, d, nt * P : (nt + 1) * P], ident[:])

                def last():
                    one(DV - 1)()
                    nc.scalar.copy(
                        out=out_v[:, nt, cols].rearrange("p (o d) -> p o d", d=DV), in_=back[:].rearrange("p d o -> p o d")
                    )
                    if nt == NODE_TILES - 1:
                        nc.sync.dma_start(
                            out=out_by_tile[:, :, O_SCAL + cols.start : O_SCAL + cols.stop], in_=out_v[:, :, cols]
                        )

                return [one(d) for d in range(DV - 1)] + [last]

            return (DV, make)

        def bypass_s(pair_ct):
            def make():
                acc = psum_acc.tile([P, 2, NODES], F32, tag="acc")

                def one(j, b, e):
                    first = (pair_ct + j) * P
                    return lambda: nc.tensor.matmul(
                        out=acc[:, j, :],
                        lhsT=b0[b][:, e, first : first + P],
                        rhs=f_t[:, b, :, e],
                        start=(b == 0 and e == 0),
                        stop=(b == FS_UNITS - 1 and e == PAIR - 1),
                    )

                steps = [one(j, b, e) for j in range(2) for b in range(FS_UNITS) for e in range(PAIR)]
                return steps[:-1] + [
                    lambda: (
                        steps[-1](),
                        nc.scalar.activation(
                            out=y_s[:, pair_ct : pair_ct + 2, :], in_=acc[:], func=ACT.Copy, scale=F_SCAL**-0.5
                        ),
                    )
                ]

            return (2 * FS_UNITS * PAIR, make)

        stats_s = small.tile([P, S_TILES, BN_STATS], F32)
        mean_var_s = small.tile([P, S_TILES, 2], F32)
        mean_w_s = small.tile([P, S_TILES], F32)
        rstd_s = small.tile([P, S_TILES], F32)
        gain_s = small.tile([P, S_TILES], F32)
        shift_s = small.tile([P, S_TILES], F32)

        def mx_s(pair_ct):
            def make():
                acc = psum_acc.tile([P, 2, NODES], F32, tag="acc")
                tiles = (pair_ct, pair_ct + 1)
                two = slice(pair_ct, pair_ct + 2)

                def one(j, g):
                    chans = slice((pair_ct + j) * P, (pair_ct + j + 1) * P)
                    return lambda: nc.tensor.matmul_mx(
                        out=acc[:, j, :],
                        lhsT=w0_codes[:, g, chans].bitcast(FP8X4),
                        lhsT_scale=w0_scales[:, g, chans],
                        rhs=h_codes[:, g, :].bitcast(FP8X4),
                        rhs_scale=h_scales[:, g, :],
                        start=(g == 0),
                        stop=(g == S_PASSES - 1),
                    )

                def last():
                    one(1, S_PASSES - 1)()
                    for j, ct in enumerate(tiles):
                        nc.vector.scalar_tensor_tensor(
                            out=y_s[:, ct, :],
                            in0=acc[:, j, :],
                            scalar=H_SCAL**-0.5,
                            in1=y_s[:, ct, :],
                            op0=ALU.mult,
                            op1=ALU.add,
                        )
                    for ct in tiles:
                        nc.vector.bn_stats(out=stats_s[:, ct, :], in_=y_s[:, ct, :])
                    for ct in tiles:
                        nc.vector.bn_aggr(out=mean_var_s[:, ct, :], in_=stats_s[:, ct, :])
                    nc.scalar.activation(
                        out=rstd_s[:, two], in_=mean_var_s[:, two, 1], func=ACT.Abs_reciprocal_sqrt, bias=eps[:]
                    )
                    nc.vector.tensor_mul(out=mean_w_s[:, two], in0=mean_var_s[:, two, 0], in1=weight_s[:, two])
                    nc.vector.tensor_mul(out=shift_s[:, two], in0=mean_w_s[:, two], in1=rstd_s[:, two])
                    nc.vector.tensor_mul(out=gain_s[:, two], in0=rstd_s[:, two], in1=weight_s[:, two])
                    nc.vector.tensor_sub(out=shift_s[:, two], in0=bias_s[:, two], in1=shift_s[:, two])
                    for ct in tiles:
                        nc.vector.tensor_scalar(
                            out=y_s[:, ct, :],
                            in0=y_s[:, ct, :],
                            scalar1=gain_s[:, ct : ct + 1],
                            scalar2=shift_s[:, ct : ct + 1],
                            op0=ALU.mult,
                            op1=ALU.add,
                        )

                return [one(j, g) for j in range(2) for g in range(S_PASSES)][:-1] + [last]

            return (2 * S_PASSES, make)

        def back_s(pair_ct):
            def make():
                back = psum_t.tile([P, NODE_TILES, 2, P], F32, tag="t")
                cols = slice(pair_ct * P, (pair_ct + 2) * P)

                def one(j, nt):
                    return lambda: nc.tensor.transpose(
                        back[:, nt, j, :], y_s[:, pair_ct + j, nt * P : (nt + 1) * P], ident[:]
                    )

                steps = [one(j, nt) for j in range(2) for nt in range(NODE_TILES)]

                def last():
                    steps[-1]()
                    nc.scalar.copy(out=out_s[:, :, cols], in_=back[:].rearrange("p nt j c -> p nt (j c)"))
                    nc.sync.dma_start(out=out_by_tile[:, :, cols], in_=out_s[:, :, cols])

                return steps[:-1] + [last]

            return (2 * NODE_TILES, make)

        pairs = range(0, S_TILES, 2)
        bypass_v_steps = [steps_of([bypass_v(ct)]) for ct in range(V_TILES)]
        bypass_s_steps = [steps_of([bypass_s(pair_ct)]) for pair_ct in pairs]

        run(steps_of([features_units(FS_UNITS + FV_BLOCKS * r, fv_words) for r in range(DV)]))

        for nt in range(NODE_TILES):
            for d in range(DV):
                copy_on("vsg"[d], hv_sorted[nt][:, d, :], hv_raw[nt][:].rearrange("p (i d) -> p d i", d=DV)[:, d, :])

        run(weave(bypass_v_steps[0] + bypass_v_steps[1], steps_of([hs_unit(g) for g in range(S_PASSES)]), 6, 4))

        bn_rows_f32 = const.tile([P, P], F32)
        nc.vector.tensor_copy(out=bn_rows_f32[:], in_=bn_rows[:])
        bn_bank = psum_t.tile([P, P], F32, tag="t")
        nc.tensor.transpose(bn_bank[:], bn_rows_f32[:], ident[:])
        bn_cols = const.tile([P, W_ROWS + B_ROWS], F32)
        nc.vector.tensor_copy(out=bn_cols[:], in_=bn_bank[:, : W_ROWS + B_ROWS])
        weight_s = bn_cols[:, 0:S_TILES]
        weight_v = bn_cols[:, S_TILES:W_ROWS]
        bias_s = bn_cols[:, W_ROWS : W_ROWS + B_ROWS]

        quantise_waiting()
        quantise_weight([(w1_raw[g][:], w1_codes[:, g, :], w1_scales[:, g, :]) for g in range(V_PASSES)])
        run(
            weave(
                bypass_v_steps[2] + bypass_v_steps[3],
                steps_of([hv_unit(g, d) for g in range(V_PASSES) for d in range(DV)]),
                4,
                4,
            )
        )
        quantise_waiting()

        run(steps_of([features_units(unit, fs_words) for unit in range(0, FS_UNITS, 2)]))
        run(bypass_s_steps[0])

        for ct in range(V_TILES):
            mx_v(ct)
            if ct % 2:
                norm_v(ct - 1)

        for g in range(S_PASSES):
            w0_pass(g)

        back_v_steps = [steps_of([back_v(ct, nt) for nt in range(NODE_TILES)]) for ct in range(V_TILES)]
        run(bypass_s_steps[1] + bypass_s_steps[2])
        run(weave(bypass_s_steps[3], back_v_steps[0] + back_v_steps[1], 4, 3))

        for pair_ct in pairs:
            run(steps_of([mx_s(pair_ct)]))
        back_s_steps = [steps_of([back_s(pair_ct)]) for pair_ct in pairs]
        run(back_v_steps[2] + back_s_steps[0] + back_v_steps[3])
        run(back_s_steps[1] + back_s_steps[2] + back_s_steps[3])
